import numpy as np
import ml_dtypes


def mxq(x, axis, fmt="e4m3"):
    dtype, down = {"e4m3": (ml_dtypes.float8_e4m3fn, 7), "e5m2": (ml_dtypes.float8_e5m2, 14)}[fmt]
    v = np.moveaxis(np.asarray(x, np.float32).astype(ml_dtypes.bfloat16).astype(np.float64), axis, -1)
    blocks = v.reshape(v.shape[:-1] + (-1, 32))
    amax = np.abs(blocks).max(-1, keepdims=True)
    byte = np.maximum(np.where(amax > 0, np.frexp(amax)[1] - 1 + 127, 0) - down, 1)
    scale = np.exp2(byte - 127.0)
    codes = (blocks / scale).astype(np.float32).astype(dtype).astype(np.float64)
    return np.moveaxis((codes * scale).reshape(v.shape), -1, axis)


WIDE = False


def mx_kscale(k):
    if not WIDE:
        return np.ones(k)
    levels = np.array([10, -10, 5, -5, 0])
    a = np.random.permutation(np.resize(levels, k // 512 * 4)).reshape(k // 512, 4)
    idx = np.arange(k)
    return np.exp2(a[idx // 512, idx % 128 // 32])


BF16 = ml_dtypes.bfloat16


def bf(x):
    return np.asarray(x, np.float32).astype(BF16)


def f64(x):
    return np.asarray(x).astype(np.float64)


E2M1 = np.array([0.0, 0.5, 1.0, 1.5, 2.0, 3.0, 4.0, 6.0, -0.0, -0.5, -1.0, -1.5, -2.0, -3.0, -4.0, -6.0])


def pack_weight(w, fmt):
    k, n = w.shape
    w = f64(bf(w)).reshape(k // 32, 32, n)
    amax = np.abs(w).max(1)
    if fmt == "e4m3":
        byte = np.frexp(amax)[1] - 1 + 127 - 7
    else:
        mant, ex = np.frexp(amax / 6.0)
        byte = np.where(mant > 0.5, ex, ex - 1) + 127
    byte = np.clip(np.where(amax > 0, byte, 1), 1, 254)
    scaled = (w * np.exp2(127.0 - byte)[:, None, :]).reshape(k, n).astype(np.float32)
    by_word = np.ascontiguousarray(scaled.reshape(k // 512, 128, 4, n).transpose(0, 1, 3, 2))
    if fmt == "e4m3":
        words = by_word.astype(ml_dtypes.float8_e4m3fn).view(np.uint8)
    else:
        c = by_word.astype(ml_dtypes.float4_e2m1fn).view(np.uint8) & 0xF
        words = c[..., 0::2] | (c[..., 1::2] << 4)
    return np.ascontiguousarray(words), np.ascontiguousarray(byte.astype(np.uint8).reshape(k // 512, 16, n))


def unpack_weight(words, scales, fmt):
    g, p, n, _ = words.shape
    if fmt == "e4m3":
        vals = np.ascontiguousarray(words).view(ml_dtypes.float8_e4m3fn).astype(np.float64)
    else:
        nib = np.empty((g, p, n, 4), np.uint8)
        nib[..., 0::2] = words & 0xF
        nib[..., 1::2] = words >> 4
        vals = E2M1[nib]
    vals = vals * np.repeat(np.exp2(scales.astype(np.float64) - 127.0), 8, axis=1)[..., None]
    return vals.transpose(0, 1, 3, 2).reshape(g * 512, n)

def pack4(w):
    words, scales = pack_weight(w, "e2m1")
    return words.reshape(words.shape[0], 128, -1), scales


def unpack4(words, scales):
    return unpack_weight(words.reshape(words.shape[0], 128, -1, 2), scales, "e2m1")


B, T, HS, WS, G, K, CB, CB2, CB3, CB4 = 2, 32, 2, 2, 8, 512, 128, 160, 200, 250
EPS = 1e-3
NV = 5
R = B * T * HS * WS


def bn_apply(v, p):
    gamma, beta, mean, var = p[0], p[1], p[2], p[3]
    return (v - mean) * (gamma / np.sqrt(var + EPS)) + beta


def dwconv_t(v, taps, d):
    vp = np.pad(v, ((0, 0), (d, d), (0, 0), (0, 0), (0, 0), (0, 0)))
    return taps[0] * vp[:, 0:T] + taps[1] * vp[:, d:d + T] + taps[2] * vp[:, 2 * d:2 * d + T]


def setup_inputs():
    s = mx_kscale(K)
    gamma = 1.0 + 0.1 * np.random.standard_normal((NV, G, CB))
    beta = 0.2 * np.random.standard_normal((NV, G, CB))
    mean = 0.04 * np.random.standard_normal((NV, G, CB))
    var = np.random.uniform(0.01, 0.04, (NV, G, CB))
    x = bf(np.random.standard_normal((B, T, HS, WS, G * K)) * np.tile(s, G))
    stack = np.random.standard_normal((NV, G, K, CB)) * 0.15 / np.sqrt(K) / s[:, None]
    words, scales = pack4(stack.reshape(-1, CB))
    return {"x": x,
            "w_words": words,
            "w_scales": scales,
            "b": bf(np.random.standard_normal((NV, G, CB)) * 0.04),
            "dw": bf(np.random.standard_normal((3, 3, G, CB)) * 0.6),
            "bn": bf(np.stack([gamma, beta, mean, var], axis=1))}


def reference(x, w_words, w_scales, b, dw, bn):
    b, dw, bn = f64(b), f64(dw), f64(bn)
    xg = f64(x).reshape(R, G, K).transpose(1, 0, 2)
    wg = unpack4(w_words, w_scales).reshape(NV, G, K, CB).transpose(1, 2, 0, 3).reshape(G, K, NV * CB)
    y = mxq(xg, 2, "e4m3") @ wg
    y = y.reshape(G, B, T, HS, WS, NV, CB).transpose(5, 1, 2, 3, 4, 0, 6) + b[:, None, None, None, None]
    outs = [bn_apply(y[0], bn[0])]
    for i, d in enumerate((1, 2, 3)):
        outs.append(bn_apply(dwconv_t(y[1 + i], dw[i], d), bn[1 + i]))
    t5 = np.maximum(y[4], np.concatenate([y[4][:, 1:], y[4][:, -1:]], axis=1))
    outs.append(bn_apply(t5, bn[4]))
    z = np.stack(outs, axis=5)
    z = np.maximum(z.reshape(B, T, HS, WS, G * NV * CB), 0.0)
    z = z.reshape(B, T, HS, WS, G, NV * CB).swapaxes(-1, -2).reshape(B, T, HS, WS, G * NV * CB)
    return z.reshape(B, T // 2, 2, HS, WS, G * NV * CB).max(axis=2)

@@ -1,0 +1,428 @@
+from contextlib import ExitStack
+
+import concourse.mybir as mybir
+from concourse.masks import make_identity
+
+F32 = mybir.dt.float32
+BF16 = mybir.dt.bfloat16
+I32 = mybir.dt.int32
+U32 = mybir.dt.uint32
+U8 = mybir.dt.uint8
+FP8X4 = mybir.dt.float8_e4m3fn_x4
+FP4X4 = mybir.dt.float4_e2m1fn_x4
+ALU = mybir.AluOpType
+ACT = mybir.ActivationFunctionType
+
+P = 128
+NB = 2
+T = 32
+S = 4
+G = 8
+K = 512
+NV = 5
+EPS = 1e-3
+FAR = 3.0e38
+COLS = T * S
+ROWS = NB * COLS
+PAIRS = G // 2
+HALF = G // 2
+
+CONV = (3, 2, 1)
+OTHER = (4, 0)
+
+FLOPS = 2 * ROWS * K * P * NV * G
+
+
+def work_order():
+    conv = [(v, pair) for v in CONV for pair in range(PAIRS)]
+    other = [(v, pair) for v in OTHER for pair in range(PAIRS)]
+    steps = conv[:PAIRS]
+    for i in range(len(other)):
+        steps.append(other[i])
+        steps.append(conv[PAIRS + i])
+    return steps
+
+
+def tile_timeception_pa_e_kernel(tc, x, w_words, w_scales, b, dw, bn, out):
+    nc = tc.nc
+    with ExitStack() as ctx:
+        keep = ctx.enter_context(tc.tile_pool(name="keep", bufs=1))
+        stage = ctx.enter_context(tc.tile_pool(name="stage", bufs=2))
+        branch = ctx.enter_context(tc.tile_pool(name="branch", bufs=4))
+        regrouped = ctx.enter_context(tc.tile_pool(name="regrouped", bufs=4))
+        fourth = ctx.enter_context(tc.tile_pool(name="fourth", bufs=2))
+        psum_t = ctx.enter_context(tc.psum_pool(name="psum_t", bufs=2))
+        psum_y = ctx.enter_context(tc.psum_pool(name="psum_y", bufs=4))
+        psum_o = ctx.enter_context(tc.psum_pool(name="psum_o", bufs=2))
+
+        one = keep.tile([P, 1], F32)
+        nc.vector.memset(one[:], 1.0)
+        rows = keep.tile([P, 3, P], BF16)
+        nc.vector.memset(rows[:, 1:3, :], 0.0)
+        bn_rows = bn.rearrange("v j g o -> (v j g) o")
+        b_rows = b.rearrange("v g o -> (v g) o")
+        dw_rows = dw.rearrange("i j g o -> (i j g) o")
+
+        def load_parameters():
+            nc.sync.dma_start(out=rows[:, 0, :], in_=bn_rows[0:P])
+            nc.sync.dma_start(out=rows[0:32, 1, :], in_=bn_rows[P : P + 32])
+            nc.sync.dma_start(out=rows[32:64, 1, :], in_=b_rows[0:32])
+            nc.sync.dma_start(out=rows[64:72, 1, :], in_=b_rows[32:40])
+            nc.sync.dma_start(out=rows[0:64, 2, :], in_=dw_rows[0:64])
+            nc.sync.dma_start(out=rows[64:72, 2, :], in_=dw_rows[64:72])
+
+        nc.scalar.activation(out=one[:], in_=one[:], func=ACT.Abs_reciprocal_sqrt)
+
+        w_planes = keep.tile([P, NV * G, P], U8, align_bytes=64)
+        nc.vector.memset(w_planes[:].bitcast(I32), 0)
+        w_sb = keep.tile([P, NV * G, 2 * P], U8, align_bytes=64)
+        words_dram = w_words.bitcast(I32)
+        scales_dram = w_scales.bitcast(I32)
+
+        def load_scales(first_branch, last_branch):
+            mats = slice(G * first_branch, G * (last_branch + 1))
+            for r in range(4):
+                nc.sync.dma_start(
+                    out=w_planes[r:P:32, mats, :].bitcast(I32),
+                    in_=scales_dram[mats, r:16:4, :].rearrange("e q c -> q e c"),
+                )
+
+        def load_words(first_branch, last_branch):
+            mats = slice(G * first_branch, G * (last_branch + 1))
+            nc.sync.dma_start(
+                out=w_sb[:, mats, :].bitcast(I32),
+                in_=words_dram[mats].rearrange("e p c -> p e c"),
+            )
+
+        x_rows = x.rearrange("n t p q c -> (t p q) n c")
+        x_sb = {}
+
+        def load_x(first_group, last_group):
+            count = last_group + 1 - first_group
+            piece = keep.tile([P, NB, K * count], BF16, name="x_sb%d" % first_group)
+            nc.sync.dma_start(
+                out=piece[:], in_=x_rows[:, :, K * first_group : K * (last_group + 1)]
+            )
+            for g in range(first_group, last_group + 1):
+                x_sb[g] = (piece, g - first_group)
+
+        load_x(0, 0)
+        load_x(1, 1)
+        load_parameters()
+        load_x(2, 3)
+        load_scales(3, 4)
+        load_words(3, 3)
+        load_x(4, 5)
+        load_x(6, 7)
+        load_scales(0, 2)
+        load_words(4, 4)
+        load_words(2, 2)
+        load_words(0, 1)
+
+        ident_bf = keep.tile([P, P], BF16)
+        make_identity(nc, ident_bf[:])
+        ident = keep.tile([P, P], F32)
+        make_identity(nc, ident[:])
+
+        par_ps = psum_o.tile([P, 3, P], BF16, tag="turned")
+        par = par_ps[:].rearrange("p c r -> p (c r)")
+        bn_par = par[:, 0 : NV * 4 * G].rearrange("p (v j g) -> p v j g", v=NV, j=4)
+        gamma = bn_par[:, :, 0, :]
+        beta = bn_par[:, :, 1, :]
+        mean = bn_par[:, :, 2, :]
+        var = bn_par[:, :, 3, :]
+        bias = par[:, 160:200].rearrange("p (v g) -> p v g", v=NV)
+        dw_par = par[:, 256:328].rearrange("p (i j g) -> p i j g", i=3, j=3)
+
+        inv_std = keep.tile([P, NV, G], F32)
+        tap_sum = keep.tile([P, NV, G], F32)
+        nc.vector.memset(tap_sum[:], 1.0)
+        offset = keep.tile([P, NV, G], F32)
+        scale = keep.tile([P, NV, G], F32)
+        spread = [P, 3, 3, G]
+        taps = keep.tile(spread, F32)
+        tap_bias = keep.tile(spread, F32)
+
+        def transpose_parameters():
+            for c in range(3):
+                nc.tensor.transpose(par_ps[:, c, :], rows[:, c, :], ident_bf[:])
+
+        def invert_std():
+            nc.scalar.activation(
+                out=inv_std[:], in_=var, func=ACT.Abs_reciprocal_sqrt, bias=EPS, scale=1.0
+            )
+
+        def before_scale():
+            nc.vector.tensor_reduce(
+                out=tap_sum[:, 1:4, :], in_=dw_par.rearrange("p i j g -> p i g j"),
+                axis=mybir.AxisListType.X, op=ALU.add,
+            )
+            nc.vector.tensor_mul(out=offset[:], in0=tap_sum[:], in1=bias)
+            nc.vector.tensor_sub(out=offset[:], in0=offset[:], in1=mean)
+
+        def after_scale():
+            nc.vector.tensor_mul(out=scale[:], in0=inv_std[:], in1=gamma)
+            nc.vector.tensor_mul(
+                out=taps[:], in0=dw_par, in1=scale[:, 1:4, :].unsqueeze(2).to_broadcast(spread)
+            )
+            nc.vector.tensor_mul(out=offset[:], in0=offset[:], in1=scale[:])
+            nc.vector.tensor_add(out=offset[:], in0=offset[:], in1=beta)
+
+        sign = keep.tile([P, G], F32)
+        even = keep.tile([P, G, NB, T // 2 + 1, S], F32)
+
+        def edge_terms():
+            nc.vector.tensor_mul(
+                out=tap_bias[:], in0=taps[:], in1=bias[:, 1:4, :].unsqueeze(2).to_broadcast(spread)
+            )
+            nc.vector.tensor_scalar(
+                out=sign[:], in0=scale[:, 4, :], scalar1=0.0, scalar2=2.0,
+                op0=ALU.is_ge, op1=ALU.mult,
+            )
+            nc.vector.tensor_scalar_add(out=sign[:], in0=sign[:], scalar1=-1.0)
+            nc.vector.tensor_scalar_mul(
+                out=even[:, :, :, T // 2, :],
+                in0=sign[:].unsqueeze(2).unsqueeze(3).to_broadcast([P, G, NB, S]),
+                scalar1=-FAR,
+            )
+
+        x_codes = keep.tile([P, G, ROWS], U32, align_bytes=64)
+        x_planes = keep.tile([P, G, ROWS], U8, align_bytes=64)
+        xt_tiles = {}
+        grouped_tiles = {}
+
+        def transpose_x(g):
+            xt = psum_t.tile([P, 2, ROWS], F32, tag="xt")
+            xt_tiles[g] = xt
+            piece, place = x_sb[g]
+            for n in range(NB):
+                words = piece[:, n, :].bitcast(F32)
+                for u in range(2):
+                    nc.tensor.transpose(
+                        xt[:, u, COLS * n : COLS * (n + 1)],
+                        words[:, (K // 2) * place + u : (K // 2) * (place + 1) : 2],
+                        ident[:],
+                    )
+
+        def regroup_x(g):
+            grouped = regrouped.tile([P, ROWS * 4], BF16, align_bytes=64)
+            grouped_tiles[g] = grouped
+            nc.scalar.copy(
+                out=grouped[:].bitcast(F32).rearrange("p (r u) -> p r u", u=2),
+                in_=xt_tiles[g][:].rearrange("p u r -> p r u"),
+            )
+
+        def quantise_x(g):
+            nc.vector.quantize_mx(
+                out=x_codes[:, g, :].bitcast(FP8X4), scales=x_planes[:, g, :],
+                in_=grouped_tiles[g][:],
+            )
+
+        steps = work_order()
+        y_tiles = {}
+        z_tiles = {}
+        results = {}
+        pooled_tiles = {}
+        turned_tiles = {}
+
+        def by_batch(ap):
+            return ap.rearrange("p (n c) -> p n c", n=NB)
+
+        def by_parity(ap, odd):
+            return ap.rearrange("p (n m two s) -> p n m two s", n=NB, two=2, s=S)[:, :, :, odd, :]
+
+        def multiply(j):
+            v, pair = steps[j]
+            y = psum_y.tile([P, 2, ROWS], F32)
+            y_tiles[j] = y
+            for i in range(2):
+                g = 2 * pair + i
+                nc.tensor.matmul_mx(
+                    out=y[:, i, :],
+                    lhsT=w_sb[:, G * v + g, :].bitcast(FP4X4),
+                    lhsT_scale=w_planes[:, G * v + g, :],
+                    rhs=x_codes[:, g, :].bitcast(FP8X4),
+                    rhs_scale=x_planes[:, g, :],
+                    start=True,
+                    stop=True,
+                )
+
+        def leave_psum(j):
+            v, pair = steps[j]
+            if v == 4:
+                for i in range(2):
+                    g = 2 * pair + i
+                    nc.scalar.activation(
+                        out=even[:, g, :, 0 : T // 2, :], in_=by_parity(y_tiles[j][:, i, :], 0),
+                        func=ACT.Copy, scale=sign[:, g : g + 1],
+                    )
+                return
+            if pair == 0:
+                z = branch.tile([P, G, ROWS], F32)
+                z_tiles[v] = z
+            for i in range(2):
+                g = 2 * pair + i
+                zg = z_tiles[v][:, g, :]
+                yg = y_tiles[j][:, i, :]
+                if v == 0:
+                    nc.scalar.activation(
+                        out=zg, in_=yg, func=ACT.Identity,
+                        scale=scale[:, v, g : g + 1], bias=offset[:, v, g : g + 1],
+                    )
+                else:
+                    nc.scalar.activation(
+                        out=zg, in_=yg, func=ACT.Identity,
+                        scale=taps[:, v - 1, 1, g : g + 1], bias=offset[:, v, g : g + 1],
+                    )
+
+        def add_tap(j, tap):
+            v, pair = steps[j]
+            w = v * S
+            for i in range(2):
+                g = 2 * pair + i
+                z_nt = by_batch(z_tiles[v][:, g, :])
+                y_nt = by_batch(y_tiles[j][:, i, :])
+                if tap == 0:
+                    target, source = z_nt[:, :, w:], y_nt[:, :, : COLS - w]
+                else:
+                    target, source = z_nt[:, :, : COLS - w], y_nt[:, :, w:]
+                nc.vector.scalar_tensor_tensor(
+                    out=target, in0=source, scalar=taps[:, v - 1, tap, g : g + 1], in1=target,
+                    op0=ALU.mult, op1=ALU.add,
+                )
+
+        window_tiles = {}
+
+        def widen(j):
+            v, pair = steps[j]
+            window = fourth.tile([P, 2, NB, T // 2, S], F32)
+            window_tiles[j] = window
+            for i in range(2):
+                g = 2 * pair + i
+                nc.vector.tensor_max(
+                    out=window[:, i], in0=even[:, g, :, 0 : T // 2, :], in1=even[:, g, :, 1 : T // 2 + 1, :]
+                )
+
+        def choose(j):
+            v, pair = steps[j]
+            if pair % 2 == 0:
+                chosen = fourth.tile([P, HALF, COLS], F32)
+                pooled_tiles[v, pair // 2] = chosen
+            for i in range(2):
+                g = 2 * pair + i
+                nc.vector.scalar_tensor_tensor(
+                    out=pooled_tiles[v, pair // 2][:, g % HALF, :].rearrange(
+                        "p (n m s) -> p n m s", n=NB, s=S
+                    ),
+                    in0=window_tiles[j][:, i], scalar=sign[:, g : g + 1],
+                    in1=by_parity(y_tiles[j][:, i, :], 1),
+                    op0=ALU.mult, op1=ALU.max,
+                )
+
+        def normalise(j):
+            v, pair = steps[j]
+            for g in (2 * pair, 2 * pair + 1):
+                chosen_g = pooled_tiles[v, pair // 2][:, g % HALF, :]
+                nc.scalar.activation(
+                    out=chosen_g, in_=chosen_g, func=ACT.Relu,
+                    scale=scale[:, v, g : g + 1], bias=offset[:, v, g : g + 1],
+                )
+
+        def finished(j):
+            if 0 <= j < len(steps) and steps[j][1] % 2 == 1:
+                return steps[j][0], steps[j][1] // 2
+            return None
+
+        def mend_edges(v, h):
+            groups = slice(HALF * h, HALF * (h + 1))
+            w = v * S
+            z_edges = z_tiles[v][:, groups, :].rearrange("p g (n c) -> p g n c", n=NB)
+            for tap, cols in ((0, slice(0, w)), (2, slice(COLS - w, COLS))):
+                extra = tap_bias[:, v - 1, tap, groups].unsqueeze(2).unsqueeze(3)
+                nc.gpsimd.tensor_tensor(
+                    out=z_edges[:, :, :, cols],
+                    in0=z_edges[:, :, :, cols],
+                    in1=extra.to_broadcast([P, HALF, NB, w]),
+                    op=ALU.subtract,
+                )
+
+        def pool_pairs(v, h):
+            groups = slice(HALF * h, HALF * (h + 1))
+            pairs = z_tiles[v][:, groups, :].rearrange("p g (m two s) -> p (g m) two s", two=2, s=S)
+            pooled = stage.tile([P, HALF, COLS], F32)
+            pooled_tiles[v, h] = pooled
+            nc.vector.scalar_tensor_tensor(
+                out=pooled[:].rearrange("p g (m s) -> p (g m) s", s=S),
+                in0=pairs[:, :, 0, :], scalar=0.0, in1=pairs[:, :, 1, :],
+                op0=ALU.max, op1=ALU.max,
+            )
+
+        def turn(v, h):
+            turned = psum_o.tile([P, HALF, P], F32, tag="turned")
+            turned_tiles[v, h] = turned
+            for i in range(HALF):
+                nc.tensor.transpose(turned[:, i, :], pooled_tiles[v, h][:, i, :], ident[:])
+
+        out_rows = out.rearrange("n t p q c -> (n t p q) c")
+
+        def shuffle_out(v, h):
+            if h == 0:
+                result = branch.tile([P, P, G], F32)
+                results[v] = result
+            nc.scalar.copy(
+                out=results[v][:, :, HALF * h : HALF * (h + 1)],
+                in_=turned_tiles[v, h][:].rearrange("p g o -> p o g"),
+            )
+            if h == 1:
+                nc.sync.dma_start(
+                    out=out_rows[:, P * G * v : P * G * (v + 1)],
+                    in_=results[v][:].rearrange("p o g -> p (o g)"),
+                )
+
+        with tc.manual_schedule():
+            transpose_x(0)
+            transpose_parameters()
+            transpose_x(1)
+            regroup_x(0)
+            invert_std()
+            regroup_x(1)
+            before_scale()
+            quantise_x(0)
+            after_scale()
+            quantise_x(1)
+            edge_terms()
+            for j in range(-3, len(steps) + 5):
+                now = steps[j] if 0 <= j < len(steps) else None
+                if now is not None and now[0] in CONV:
+                    add_tap(j, 0)
+                if now is not None and now[0] == 4:
+                    widen(j)
+                if finished(j - 1) is not None and finished(j - 1)[0] in CONV:
+                    mend_edges(*finished(j - 1))
+                if finished(j - 2) is not None and finished(j - 2)[0] != 4:
+                    pool_pairs(*finished(j - 2))
+                if now is not None and now[0] in CONV:
+                    add_tap(j, 2)
+                if now is not None and now[0] == 4:
+                    choose(j)
+                if 1 <= j + 2 < PAIRS:
+                    quantise_x(2 * (j + 2))
+                    quantise_x(2 * (j + 2) + 1)
+
+                if 0 <= j + 2 < len(steps):
+                    multiply(j + 2)
+                if finished(j - 3) is not None:
+                    turn(*finished(j - 3))
+                if 1 <= j + 4 < PAIRS:
+                    transpose_x(2 * (j + 4))
+                    transpose_x(2 * (j + 4) + 1)
+
+                if 0 <= j + 1 < len(steps):
+                    leave_psum(j + 1)
+                if 1 <= j + 3 < PAIRS:
+                    regroup_x(2 * (j + 3))
+                    regroup_x(2 * (j + 3) + 1)
+                if 0 <= j - 1 < len(steps) and steps[j - 1][0] == 4:
+                    normalise(j - 1)
+                if finished(j - 4) is not None:
+                    shuffle_out(*finished(j - 4))

@@ -22,24 +22,27 @@ K = 512
 NV = 5
 EPS = 1e-3
 FAR = 3.0e38
-COLS = T * S
-ROWS = NB * COLS
+ROWS = NB * T * S
+STEP = S * NB
+OUT_T = T // 2
+COLS = OUT_T * STEP
 PAIRS = G // 2
 HALF = G // 2
 
+TURNED_CONV = (3, 1)
+FIRST, STRIDE, MERGE = 4, 2, 20
+PAD = 2
+
 CONV = (3, 2, 1)
-OTHER = (4, 0)
 
 FLOPS = 2 * ROWS * K * P * NV * G
 
 
 def work_order():
-    conv = [(v, pair) for v in CONV for pair in range(PAIRS)]
-    other = [(v, pair) for v in OTHER for pair in range(PAIRS)]
-    steps = conv[:PAIRS]
-    for i in range(len(other)):
-        steps.append(other[i])
-        steps.append(conv[PAIRS + i])
+    steps = [(3, pair) for pair in range(PAIRS)]
+    for first, second in ((4, 2), (1, 0)):
+        for pair in range(PAIRS):
+            steps += [(first, pair), (second, pair)]
     return steps
 
 
@@ -48,28 +51,26 @@ def tile_timeception_pa_e_kernel(tc, x, w_words, w_scales, b, dw, bn, out):
     with ExitStack() as ctx:
         keep = ctx.enter_context(tc.tile_pool(name="keep", bufs=1))
         stage = ctx.enter_context(tc.tile_pool(name="stage", bufs=2))
-        branch = ctx.enter_context(tc.tile_pool(name="branch", bufs=4))
+        branch = ctx.enter_context(tc.tile_pool(name="branch", bufs=3))
+        outcome = ctx.enter_context(tc.tile_pool(name="outcome", bufs=NV))
         regrouped = ctx.enter_context(tc.tile_pool(name="regrouped", bufs=4))
         fourth = ctx.enter_context(tc.tile_pool(name="fourth", bufs=2))
+        merged = ctx.enter_context(tc.tile_pool(name="merged", bufs=1))
         psum_t = ctx.enter_context(tc.psum_pool(name="psum_t", bufs=2))
         psum_y = ctx.enter_context(tc.psum_pool(name="psum_y", bufs=4))
         psum_o = ctx.enter_context(tc.psum_pool(name="psum_o", bufs=2))
 
         one = keep.tile([P, 1], F32)
         nc.vector.memset(one[:], 1.0)
-        rows = keep.tile([P, 3, P], BF16)
-        nc.vector.memset(rows[:, 1:3, :], 0.0)
-        bn_rows = bn.rearrange("v j g o -> (v j g) o")
-        b_rows = b.rearrange("v g o -> (v g) o")
-        dw_rows = dw.rearrange("i j g o -> (i j g) o")
+        rows = keep.tile([P, NV, P], BF16)
+        nc.vector.memset(rows[:].bitcast(I32), 0)
 
         def load_parameters():
-            nc.sync.dma_start(out=rows[:, 0, :], in_=bn_rows[0:P])
-            nc.sync.dma_start(out=rows[0:32, 1, :], in_=bn_rows[P : P + 32])
-            nc.sync.dma_start(out=rows[32:64, 1, :], in_=b_rows[0:32])
-            nc.sync.dma_start(out=rows[64:72, 1, :], in_=b_rows[32:40])
-            nc.sync.dma_start(out=rows[0:64, 2, :], in_=dw_rows[0:64])
-            nc.sync.dma_start(out=rows[64:72, 2, :], in_=dw_rows[64:72])
+            nc.sync.dma_start(out=rows[0:32], in_=bn.rearrange("v j g o -> (j g) v o"))
+            nc.sync.dma_start(out=rows[32:40], in_=b.rearrange("v g o -> g v o"))
+            dw_rows = dw.rearrange("i j g o -> (j g) i o")
+            nc.sync.dma_start(out=rows[64:80, 0:3, :], in_=dw_rows[0:16])
+            nc.sync.dma_start(out=rows[80:88, 0:3, :], in_=dw_rows[16:24])
 
         nc.scalar.activation(out=one[:], in_=one[:], func=ACT.Abs_reciprocal_sqrt)
 
@@ -87,8 +88,8 @@ def tile_timeception_pa_e_kernel(tc, x, w_words, w_scales, b, dw, bn, out):
                     in_=scales_dram[mats, r:16:4, :].rearrange("e q c -> q e c"),
                 )
 
-        def load_words(first_branch, last_branch):
-            mats = slice(G * first_branch, G * (last_branch + 1))
+        def load_words(first, last):
+            mats = slice(first, last)
             nc.sync.dma_start(
                 out=w_sb[:, mats, :].bitcast(I32),
                 in_=words_dram[mats].rearrange("e p c -> p e c"),
@@ -107,32 +108,32 @@ def tile_timeception_pa_e_kernel(tc, x, w_words, w_scales, b, dw, bn, out):
                 x_sb[g] = (piece, g - first_group)
 
         load_x(0, 0)
-        load_x(1, 1)
         load_parameters()
+        load_x(1, 1)
         load_x(2, 3)
         load_scales(3, 4)
-        load_words(3, 3)
+        load_words(3 * G, 3 * G + 2)
+        load_words(3 * G + 2, 4 * G)
         load_x(4, 5)
         load_x(6, 7)
         load_scales(0, 2)
-        load_words(4, 4)
-        load_words(2, 2)
-        load_words(0, 1)
+        load_words(4 * G, 5 * G)
+        load_words(2 * G, 3 * G)
+        load_words(0, 2 * G)
 
         ident_bf = keep.tile([P, P], BF16)
         make_identity(nc, ident_bf[:])
         ident = keep.tile([P, P], F32)
         make_identity(nc, ident[:])
 
-        par_ps = psum_o.tile([P, 3, P], BF16, tag="turned")
-        par = par_ps[:].rearrange("p c r -> p (c r)")
-        bn_par = par[:, 0 : NV * 4 * G].rearrange("p (v j g) -> p v j g", v=NV, j=4)
+        par_ps = psum_o.tile([P, NV, P], BF16, tag="turned")
+        bn_par = par_ps[:, :, 0:32].rearrange("p v (j g) -> p v j g", j=4)
         gamma = bn_par[:, :, 0, :]
         beta = bn_par[:, :, 1, :]
         mean = bn_par[:, :, 2, :]
         var = bn_par[:, :, 3, :]
-        bias = par[:, 160:200].rearrange("p (v g) -> p v g", v=NV)
-        dw_par = par[:, 256:328].rearrange("p (i j g) -> p i j g", i=3, j=3)
+        bias = par_ps[:, :, 32:40]
+        dw_par = par_ps[:, 0:3, 64:88].rearrange("p i (j g) -> p i j g", j=3)
 
         inv_std = keep.tile([P, NV, G], F32)
         tap_sum = keep.tile([P, NV, G], F32)
@@ -144,7 +145,7 @@ def tile_timeception_pa_e_kernel(tc, x, w_words, w_scales, b, dw, bn, out):
         tap_bias = keep.tile(spread, F32)
 
         def transpose_parameters():
-            for c in range(3):
+            for c in range(NV):
                 nc.tensor.transpose(par_ps[:, c, :], rows[:, c, :], ident_bf[:])
 
         def invert_std():
@@ -169,7 +170,7 @@ def tile_timeception_pa_e_kernel(tc, x, w_words, w_scales, b, dw, bn, out):
             nc.vector.tensor_add(out=offset[:], in0=offset[:], in1=beta)
 
         sign = keep.tile([P, G], F32)
-        even = keep.tile([P, G, NB, T // 2 + 1, S], F32)
+        even = keep.tile([P, G, OUT_T + 1, STEP], F32)
 
         def edge_terms():
             nc.vector.tensor_mul(
@@ -181,10 +182,33 @@ def tile_timeception_pa_e_kernel(tc, x, w_words, w_scales, b, dw, bn, out):
             )
             nc.vector.tensor_scalar_add(out=sign[:], in0=sign[:], scalar1=-1.0)
             nc.vector.tensor_scalar_mul(
-                out=even[:, :, :, T // 2, :],
-                in0=sign[:].unsqueeze(2).unsqueeze(3).to_broadcast([P, G, NB, S]),
+                out=even[:, :, OUT_T, :],
+                in0=sign[:].unsqueeze(2).to_broadcast([P, G, STEP]),
                 scalar1=-FAR,
             )
+
+        turned_v, turned_h = TURNED_CONV
+        turned_groups = slice(HALF * turned_h, HALF * (turned_h + 1))
+        diag = keep.tile([P, 3, HALF, P], F32)
+        padded = keep.tile([P, HALF, 2, OUT_T + 2 * PAD, STEP], F32)
+        nc.gpsimd.memset(padded[:, :, :, 0:PAD, :], 0.0)
+        nc.gpsimd.memset(padded[:, :, :, PAD + OUT_T :, :], 0.0)
+        own_bias = keep.tile([P, HALF], F32)
+        shift = keep.tile([P, HALF], F32)
+
+        def turned_constants():
+            nc.vector.tensor_copy(out=own_bias[:], in_=bias[:, turned_v, turned_groups])
+            nc.vector.tensor_mul(
+                out=shift[:], in0=scale[:, turned_v, turned_groups], in1=mean[:, turned_v, turned_groups]
+            )
+            for tap in range(3):
+                for i in range(HALF):
+                    g = HALF * turned_h + i
+                    nc.gpsimd.tensor_scalar(
+                        out=diag[:, tap, i, :], in0=ident[:], scalar1=taps[:, turned_v - 1, tap, g : g + 1],
+                        scalar2=0.0, op0=ALU.mult, op1=ALU.add,
+                    )
+            nc.vector.tensor_sub(out=shift[:], in0=beta[:, turned_v, turned_groups], in1=shift[:])
 
         x_codes = keep.tile([P, G, ROWS], U32, align_bytes=64)
         x_planes = keep.tile([P, G, ROWS], U8, align_bytes=64)
@@ -199,7 +223,7 @@ def tile_timeception_pa_e_kernel(tc, x, w_words, w_scales, b, dw, bn, out):
                 words = piece[:, n, :].bitcast(F32)
                 for u in range(2):
                     nc.tensor.transpose(
-                        xt[:, u, COLS * n : COLS * (n + 1)],
+                        xt[:, u, P * n : P * (n + 1)],
                         words[:, (K // 2) * place + u : (K // 2) * (place + 1) : 2],
                         ident[:],
                     )
@@ -208,8 +232,8 @@ def tile_timeception_pa_e_kernel(tc, x, w_words, w_scales, b, dw, bn, out):
             grouped = regrouped.tile([P, ROWS * 4], BF16, align_bytes=64)
             grouped_tiles[g] = grouped
             nc.scalar.copy(
-                out=grouped[:].bitcast(F32).rearrange("p (r u) -> p r u", u=2),
-                in_=xt_tiles[g][:].rearrange("p u r -> p r u"),
+                out=grouped[:].bitcast(F32).rearrange("p (c n u) -> p c n u", n=NB, u=2),
+                in_=xt_tiles[g][:].rearrange("p u (n c) -> p c n u", n=NB),
             )
 
         def quantise_x(g):
@@ -225,11 +249,8 @@ def tile_timeception_pa_e_kernel(tc, x, w_words, w_scales, b, dw, bn, out):
         pooled_tiles = {}
         turned_tiles = {}
 
-        def by_batch(ap):
-            return ap.rearrange("p (n c) -> p n c", n=NB)
-
         def by_parity(ap, odd):
-            return ap.rearrange("p (n m two s) -> p n m two s", n=NB, two=2, s=S)[:, :, :, odd, :]
+            return ap.rearrange("p (m two c) -> p m two c", two=2, c=STEP)[:, :, odd, :]
 
         def multiply(j):
             v, pair = steps[j]
@@ -249,58 +270,86 @@ def tile_timeception_pa_e_kernel(tc, x, w_words, w_scales, b, dw, bn, out):
 
         def leave_psum(j):
             v, pair = steps[j]
+            if v == 0:
+                scaled = fourth.tile([P, 2, OUT_T, STEP], F32)
+                scaled_tiles[j] = scaled
+                for i in range(2):
+                    g = 2 * pair + i
+                    nc.scalar.activation(
+                        out=scaled[:, i], in_=by_parity(y_tiles[j][:, i, :], 0),
+                        func=ACT.Copy, scale=scale[:, v, g : g + 1],
+                    )
+                return
             if v == 4:
                 for i in range(2):
                     g = 2 * pair + i
                     nc.scalar.activation(
-                        out=even[:, g, :, 0 : T // 2, :], in_=by_parity(y_tiles[j][:, i, :], 0),
+                        out=even[:, g, 0:OUT_T, :], in_=by_parity(y_tiles[j][:, i, :], 0),
                         func=ACT.Copy, scale=sign[:, g : g + 1],
                     )
                 return
-            if pair == 0:
+            if (v, pair // 2) == TURNED_CONV:
+                for i in range(2):
+                    place = 2 * (pair % 2) + i
+                    nc.scalar.activation(
+                        out=padded[:, place, :, PAD : PAD + OUT_T, :],
+                        in_=y_tiles[j][:, i, :].rearrange("p (m two c) -> p two m c", two=2, c=STEP),
+                        func=ACT.Identity, bias=own_bias[:, place : place + 1], scale=1.0,
+                    )
+                return
+            if v not in z_tiles:
                 z = branch.tile([P, G, ROWS], F32)
                 z_tiles[v] = z
             for i in range(2):
                 g = 2 * pair + i
                 zg = z_tiles[v][:, g, :]
                 yg = y_tiles[j][:, i, :]
-                if v == 0:
-                    nc.scalar.activation(
-                        out=zg, in_=yg, func=ACT.Identity,
-                        scale=scale[:, v, g : g + 1], bias=offset[:, v, g : g + 1],
-                    )
-                else:
-                    nc.scalar.activation(
-                        out=zg, in_=yg, func=ACT.Identity,
-                        scale=taps[:, v - 1, 1, g : g + 1], bias=offset[:, v, g : g + 1],
-                    )
+                nc.scalar.activation(
+                    out=zg, in_=yg, func=ACT.Identity,
+                    scale=taps[:, v - 1, 1, g : g + 1], bias=offset[:, v, g : g + 1],
+                )
 
         def add_tap(j, tap):
             v, pair = steps[j]
-            w = v * S
+            w = v * STEP
             for i in range(2):
                 g = 2 * pair + i
-                z_nt = by_batch(z_tiles[v][:, g, :])
-                y_nt = by_batch(y_tiles[j][:, i, :])
                 if tap == 0:
-                    target, source = z_nt[:, :, w:], y_nt[:, :, : COLS - w]
+                    target, source = z_tiles[v][:, g, w:], y_tiles[j][:, i, : ROWS - w]
                 else:
-                    target, source = z_nt[:, :, : COLS - w], y_nt[:, :, w:]
+                    target, source = z_tiles[v][:, g, : ROWS - w], y_tiles[j][:, i, w:]
                 nc.vector.scalar_tensor_tensor(
                     out=target, in0=source, scalar=taps[:, v - 1, tap, g : g + 1], in1=target,
                     op0=ALU.mult, op1=ALU.add,
                 )
 
         window_tiles = {}
+        scaled_tiles = {}
+
+        def pool_plain(j):
+            v, pair = steps[j]
+            if pair % 2 == 0:
+                chosen = fourth.tile([P, HALF, COLS], F32)
+                pooled_tiles[v, pair // 2] = chosen
+            for i in range(2):
+                g = 2 * pair + i
+                nc.vector.scalar_tensor_tensor(
+                    out=pooled_tiles[v, pair // 2][:, g % HALF, :].rearrange(
+                        "p (m c) -> p m c", c=STEP
+                    ),
+                    in0=by_parity(y_tiles[j][:, i, :], 1), scalar=scale[:, v, g : g + 1],
+                    in1=scaled_tiles[j][:, i],
+                    op0=ALU.mult, op1=ALU.max,
+                )
 
         def widen(j):
             v, pair = steps[j]
-            window = fourth.tile([P, 2, NB, T // 2, S], F32)
+            window = fourth.tile([P, 2, OUT_T, STEP], F32)
             window_tiles[j] = window
             for i in range(2):
                 g = 2 * pair + i
                 nc.vector.tensor_max(
-                    out=window[:, i], in0=even[:, g, :, 0 : T // 2, :], in1=even[:, g, :, 1 : T // 2 + 1, :]
+                    out=window[:, i], in0=even[:, g, 0:OUT_T, :], in1=even[:, g, 1 : OUT_T + 1, :]
                 )
 
         def choose(j):
@@ -312,7 +361,7 @@ def tile_timeception_pa_e_kernel(tc, x, w_words, w_scales, b, dw, bn, out):
                 g = 2 * pair + i
                 nc.vector.scalar_tensor_tensor(
                     out=pooled_tiles[v, pair // 2][:, g % HALF, :].rearrange(
-                        "p (n m s) -> p n m s", n=NB, s=S
+                        "p (m c) -> p m c", c=STEP
                     ),
                     in0=window_tiles[j][:, i], scalar=sign[:, g : g + 1],
                     in1=by_parity(y_tiles[j][:, i, :], 1),
@@ -330,29 +379,29 @@ def tile_timeception_pa_e_kernel(tc, x, w_words, w_scales, b, dw, bn, out):
 
         def finished(j):
             if 0 <= j < len(steps) and steps[j][1] % 2 == 1:
-                return steps[j][0], steps[j][1] // 2
+                half = steps[j][0], steps[j][1] // 2
+                return None if half == TURNED_CONV else half
             return None
 
         def mend_edges(v, h):
             groups = slice(HALF * h, HALF * (h + 1))
-            w = v * S
-            z_edges = z_tiles[v][:, groups, :].rearrange("p g (n c) -> p g n c", n=NB)
-            for tap, cols in ((0, slice(0, w)), (2, slice(COLS - w, COLS))):
-                extra = tap_bias[:, v - 1, tap, groups].unsqueeze(2).unsqueeze(3)
+            w = v * STEP
+            for tap, cols in ((0, slice(0, w)), (2, slice(ROWS - w, ROWS))):
+                extra = tap_bias[:, v - 1, tap, groups].unsqueeze(2)
                 nc.gpsimd.tensor_tensor(
-                    out=z_edges[:, :, :, cols],
-                    in0=z_edges[:, :, :, cols],
-                    in1=extra.to_broadcast([P, HALF, NB, w]),
+                    out=z_tiles[v][:, groups, cols],
+                    in0=z_tiles[v][:, groups, cols],
+                    in1=extra.to_broadcast([P, HALF, w]),
                     op=ALU.subtract,
                 )
 
         def pool_pairs(v, h):
             groups = slice(HALF * h, HALF * (h + 1))
-            pairs = z_tiles[v][:, groups, :].rearrange("p g (m two s) -> p (g m) two s", two=2, s=S)
+            pairs = z_tiles[v][:, groups, :].rearrange("p g (m two c) -> p (g m) two c", two=2, c=STEP)
             pooled = stage.tile([P, HALF, COLS], F32)
             pooled_tiles[v, h] = pooled
             nc.vector.scalar_tensor_tensor(
-                out=pooled[:].rearrange("p g (m s) -> p (g m) s", s=S),
+                out=pooled[:].rearrange("p g (m c) -> p (g m) c", c=STEP),
                 in0=pairs[:, :, 0, :], scalar=0.0, in1=pairs[:, :, 1, :],
                 op0=ALU.max, op1=ALU.max,
             )
@@ -361,23 +410,92 @@ def tile_timeception_pa_e_kernel(tc, x, w_words, w_scales, b, dw, bn, out):
             turned = psum_o.tile([P, HALF, P], F32, tag="turned")
             turned_tiles[v, h] = turned
             for i in range(HALF):
-                nc.tensor.transpose(turned[:, i, :], pooled_tiles[v, h][:, i, :], ident[:])
+                if v == 0:
+                    g = HALF * h + i
+                    nc.tensor.matmul(
+                        turned[:, i, :], lhsT=pooled_tiles[v, h][:, i, :], rhs=ident[:],
+                        is_transpose=True, start=True, stop=False,
+                    )
+                    nc.tensor.matmul(
+                        turned[:, i, :], lhsT=offset[:, v, g : g + 1].to_broadcast([P, P]), rhs=ident[:],
+                        is_transpose=True, start=False, stop=True,
+                    )
+                else:
+                    nc.tensor.transpose(turned[:, i, :], pooled_tiles[v, h][:, i, :], ident[:])
 
-        out_rows = out.rearrange("n t p q c -> (n t p q) c")
+        out_rows = out.rearrange("n t p q c -> n (t p q) c")
+
+        parity_tiles = {}
+        relu_tiles = {}
+
+        def convolve_turned(k):
+            i, parity = k // 2, k % 2
+            if i == 0:
+                parity_tile = psum_t.tile([P, HALF, P], F32, tag="xt")
+                parity_tiles[parity] = parity_tile
+            target = parity_tiles[parity][:, i, :]
+            for tap in range(3):
+                from_first = parity + (tap - 1) * turned_v
+                first = (PAD + from_first // 2) * STEP
+                source = padded[:, i, from_first % 2].rearrange("p m c -> p (m c)")
+                nc.tensor.matmul(
+                    target, lhsT=source[:, first : first + COLS], rhs=diag[:, tap, i, :],
+                    start=(tap == 0), stop=False,
+                )
+            nc.tensor.matmul(
+                target, lhsT=shift[:, i : i + 1].to_broadcast([P, P]), rhs=ident[:],
+                is_transpose=True, start=False, stop=True,
+            )
+
+        def relu_even():
+            relu = merged.tile([P, P, HALF], F32)
+            relu_tiles[0] = relu
+            nc.scalar.activation(
+                out=relu[:], in_=parity_tiles[0][:].rearrange("p g o -> p o g"), func=ACT.Relu
+            )
+
+        halves_in = []
+
+        def store_when_whole(v):
+            halves_in.append(v)
+            if halves_in.count(v) == 2:
+                for n in range(NB):
+                    nc.sync.dma_start(
+                        out=out_rows[n, :, P * G * v : P * G * (v + 1)],
+                        in_=results[v][n:P:NB].rearrange("p o g -> p (o g)"),
+                    )
+
+        def merge_odd():
+            if turned_v not in results:
+                result = outcome.tile([P, P, G], F32)
+                results[turned_v] = result
+            nc.vector.tensor_max(
+                out=results[turned_v][:, :, turned_groups],
+                in0=parity_tiles[1][:].rearrange("p g o -> p o g"), in1=relu_tiles[0][:],
+            )
+            store_when_whole(turned_v)
 
         def shuffle_out(v, h):
-            if h == 0:
-                result = branch.tile([P, P, G], F32)
+            if v not in results:
+                result = outcome.tile([P, P, G], F32)
                 results[v] = result
-            nc.scalar.copy(
+            nc.scalar.activation(
                 out=results[v][:, :, HALF * h : HALF * (h + 1)],
                 in_=turned_tiles[v, h][:].rearrange("p g o -> p o g"),
+                func=ACT.Relu,
             )
-            if h == 1:
-                nc.sync.dma_start(
-                    out=out_rows[:, P * G * v : P * G * (v + 1)],
-                    in_=results[v][:].rearrange("p o g -> p (o g)"),
-                )
+            store_when_whole(v)
+
+        def is_tapped(j):
+            return steps[j][0] in CONV and (steps[j][0], steps[j][1] // 2) != TURNED_CONV
+
+        def turned_now(j):
+            found = []
+            for lag in (3, 2, 1):
+                half = finished(j - lag)
+                if half is not None and lag == {0: 1, 4: 2}.get(half[0], 3):
+                    found.append(half)
+            return found
 
         with tc.manual_schedule():
             transpose_x(0)
@@ -391,28 +509,35 @@ def tile_timeception_pa_e_kernel(tc, x, w_words, w_scales, b, dw, bn, out):
             after_scale()
             quantise_x(1)
             edge_terms()
+            turned_constants()
             for j in range(-3, len(steps) + 5):
                 now = steps[j] if 0 <= j < len(steps) else None
-                if now is not None and now[0] in CONV:
+                if now is not None and is_tapped(j):
                     add_tap(j, 0)
                 if now is not None and now[0] == 4:
                     widen(j)
                 if finished(j - 1) is not None and finished(j - 1)[0] in CONV:
                     mend_edges(*finished(j - 1))
-                if finished(j - 2) is not None and finished(j - 2)[0] != 4:
+                if finished(j - 2) is not None and finished(j - 2)[0] in CONV:
                     pool_pairs(*finished(j - 2))
-                if now is not None and now[0] in CONV:
+                if now is not None and is_tapped(j):
                     add_tap(j, 2)
                 if now is not None and now[0] == 4:
                     choose(j)
+                if now is not None and now[0] == 0:
+                    pool_plain(j)
+                if j == MERGE:
+                    merge_odd()
                 if 1 <= j + 2 < PAIRS:
                     quantise_x(2 * (j + 2))
                     quantise_x(2 * (j + 2) + 1)
 
                 if 0 <= j + 2 < len(steps):
                     multiply(j + 2)
-                if finished(j - 3) is not None:
-                    turn(*finished(j - 3))
+                for half in turned_now(j):
+                    turn(*half)
+                if FIRST <= j < FIRST + 2 * HALF * STRIDE and (j - FIRST) % STRIDE == 0:
+                    convolve_turned((j - FIRST) // STRIDE)
                 if 1 <= j + 4 < PAIRS:
                     transpose_x(2 * (j + 4))
                     transpose_x(2 * (j + 4) + 1)
@@ -424,5 +549,7 @@ def tile_timeception_pa_e_kernel(tc, x, w_words, w_scales, b, dw, bn, out):
                     regroup_x(2 * (j + 3) + 1)
                 if 0 <= j - 1 < len(steps) and steps[j - 1][0] == 4:
                     normalise(j - 1)
-                if finished(j - 4) is not None:
-                    shuffle_out(*finished(j - 4))
+                if j == MERGE - 1:
+                    relu_even()
+                for half in turned_now(j - 1):
+                    shuffle_out(*half)

@@ -29,9 +29,15 @@ COLS = OUT_T * STEP
 PAIRS = G // 2
 HALF = G // 2
 
-TURNED_CONV = (3, 1)
-FIRST, STRIDE, MERGE = 4, 2, 20
-PAD = 2
+DIAGONAL = (9, 9)
+SCALED = ((3, 1), (1, 0),)
+TURNED = ((3, 1), (1, 0),)
+PIECES = {9: [((3, 1), 0), ((3, 1), 1), ((3, 1), 2), ((3, 1), 3)], 10: [((3, 1), 4), ((3, 1), 5), ((3, 1), 6), ((3, 1), 7)], 17: [((1, 0), 0), ((1, 0), 1), ((1, 0), 2), ((1, 0), 3)], 18: [((1, 0), 4), ((1, 0), 5), ((1, 0), 6), ((1, 0), 7)]}
+MERGE = {(3, 1): 12, (1, 0): 20}
+RELU = {(3, 1): 11, (1, 0): 19}
+CENTRE = {(3, 1): "vector", (1, 0): "vector"}
+PRODUCTS = {3: [((3, 1), 0), ((3, 1), 1), ((3, 1), 2)], 4: [((3, 1), 3), ((3, 1), 4), ((3, 1), 5)], 5: [((3, 1), 6), ((3, 1), 7), ((3, 1), 8)], 6: [((3, 1), 9), ((3, 1), 10), ((3, 1), 11)], 13: [((1, 0), 0), ((1, 0), 1), ((1, 0), 2)], 14: [((1, 0), 3), ((1, 0), 4), ((1, 0), 5)], 15: [((1, 0), 6), ((1, 0), 7), ((1, 0), 8)], 16: [((1, 0), 9), ((1, 0), 10), ((1, 0), 11)]}
+HALVES = tuple((v, h) for v in range(5) for h in range(2))
 
 CONV = (3, 2, 1)
 
@@ -55,8 +61,8 @@ def tile_timeception_pa_e_kernel(tc, x, w_words, w_scales, b, dw, bn, out):
         outcome = ctx.enter_context(tc.tile_pool(name="outcome", bufs=NV))
         regrouped = ctx.enter_context(tc.tile_pool(name="regrouped", bufs=4))
         fourth = ctx.enter_context(tc.tile_pool(name="fourth", bufs=2))
-        merged = ctx.enter_context(tc.tile_pool(name="merged", bufs=1))
-        psum_t = ctx.enter_context(tc.psum_pool(name="psum_t", bufs=2))
+        merged = ctx.enter_context(tc.tile_pool(name="merged", bufs=2))
+        psum_x = ctx.enter_context(tc.psum_pool(name="psum_x", bufs=2))
         psum_y = ctx.enter_context(tc.psum_pool(name="psum_y", bufs=4))
         psum_o = ctx.enter_context(tc.psum_pool(name="psum_o", bufs=2))
 
@@ -113,8 +119,8 @@ def tile_timeception_pa_e_kernel(tc, x, w_words, w_scales, b, dw, bn, out):
         load_x(2, 3)
         load_scales(3, 4)
         load_words(3 * G, 3 * G + 2)
-        load_words(3 * G + 2, 4 * G)
         load_x(4, 5)
+        load_words(3 * G + 2, 4 * G)
         load_x(6, 7)
         load_scales(0, 2)
         load_words(4 * G, 5 * G)
@@ -126,7 +132,7 @@ def tile_timeception_pa_e_kernel(tc, x, w_words, w_scales, b, dw, bn, out):
         ident = keep.tile([P, P], F32)
         make_identity(nc, ident[:])
 
-        par_ps = psum_o.tile([P, NV, P], BF16, tag="turned")
+        par_ps = psum_y.tile([P, NV, P], BF16, tag="y")
         bn_par = par_ps[:, :, 0:32].rearrange("p v (j g) -> p v j g", j=4)
         gamma = bn_par[:, :, 0, :]
         beta = bn_par[:, :, 1, :]
@@ -187,28 +193,46 @@ def tile_timeception_pa_e_kernel(tc, x, w_words, w_scales, b, dw, bn, out):
                 scalar1=-FAR,
             )
 
-        turned_v, turned_h = TURNED_CONV
-        turned_groups = slice(HALF * turned_h, HALF * (turned_h + 1))
-        diag = keep.tile([P, 3, HALF, P], F32)
-        padded = keep.tile([P, HALF, 2, OUT_T + 2 * PAD, STEP], F32)
-        nc.gpsimd.memset(padded[:, :, :, 0:PAD, :], 0.0)
-        nc.gpsimd.memset(padded[:, :, :, PAD + OUT_T :, :], 0.0)
-        own_bias = keep.tile([P, HALF], F32)
-        shift = keep.tile([P, HALF], F32)
+        PAD = {half: (half[0] + 1) // 2 for half in TURNED}
+        padded = {}
+        for half in TURNED:
+            pad = PAD[half]
+            tile = keep.tile([P, HALF, 2, OUT_T + 2 * pad, STEP], F32, name="padded%d%d" % half)
+            padded[half] = tile
+            nc.gpsimd.memset(tile[:, :, :, 0:pad, :], 0.0)
+            nc.gpsimd.memset(tile[:, :, :, pad + OUT_T :, :], 0.0)
+        diag = None
+        product = {}
+        for half in SCALED:
+            tile = keep.tile([P, 3, HALF, 2, (OUT_T + 2 * PAD[half]) * STEP], F32, name="product%d%d" % half)
+            product[half] = tile
+        own_bias = keep.tile([P, NV, G], F32)
+        shift = keep.tile([P, NV, G], F32)
+        centre_offset = keep.tile([P, NV, G], F32)
 
         def turned_constants():
-            nc.vector.tensor_copy(out=own_bias[:], in_=bias[:, turned_v, turned_groups])
-            nc.vector.tensor_mul(
-                out=shift[:], in0=scale[:, turned_v, turned_groups], in1=mean[:, turned_v, turned_groups]
-            )
-            for tap in range(3):
-                for i in range(HALF):
-                    g = HALF * turned_h + i
+            nc.vector.tensor_copy(out=own_bias[:], in_=bias)
+            nc.vector.tensor_mul(out=shift[:], in0=scale[:], in1=mean)
+            v, h = DIAGONAL
+            for i in range(HALF if DIAGONAL in TURNED else 0):
+                g = HALF * h + i
+                for tap in range(3):
                     nc.gpsimd.tensor_scalar(
-                        out=diag[:, tap, i, :], in0=ident[:], scalar1=taps[:, turned_v - 1, tap, g : g + 1],
+                        out=diag[:, tap, i, :], in0=ident[:], scalar1=taps[:, v - 1, tap, g : g + 1],
                         scalar2=0.0, op0=ALU.mult, op1=ALU.add,
                     )
-            nc.vector.tensor_sub(out=shift[:], in0=beta[:, turned_v, turned_groups], in1=shift[:])
+            nc.vector.tensor_sub(out=shift[:], in0=beta, in1=shift[:])
+            nc.vector.tensor_add(out=centre_offset[:, 1:4, :], in0=shift[:, 1:4, :], in1=tap_bias[:, :, 1, :])
+
+        def scale_tap(half, n, engine):
+            v, h = half
+            i, tap = n // 3, n % 3
+            g = HALF * h + i
+            engine.tensor_scalar(
+                out=product[half][:, tap, i], in0=padded[half][:, i].rearrange("p two m c -> p two (m c)"),
+                scalar1=taps[:, v - 1, tap, g : g + 1],
+                scalar2=shift[:, v, g : g + 1] if tap == 1 else 0.0, op0=ALU.mult, op1=ALU.add,
+            )
 
         x_codes = keep.tile([P, G, ROWS], U32, align_bytes=64)
         x_planes = keep.tile([P, G, ROWS], U8, align_bytes=64)
@@ -216,7 +240,10 @@ def tile_timeception_pa_e_kernel(tc, x, w_words, w_scales, b, dw, bn, out):
         grouped_tiles = {}
 
         def transpose_x(g):
-            xt = psum_t.tile([P, 2, ROWS], F32, tag="xt")
+            if g % 4 < 2:
+                xt = psum_x.tile([P, 2, ROWS], F32, tag="xt")
+            else:
+                xt = psum_o.tile([P, 2, ROWS], F32, tag="turned")
             xt_tiles[g] = xt
             piece, place = x_sb[g]
             for n in range(NB):
@@ -232,6 +259,14 @@ def tile_timeception_pa_e_kernel(tc, x, w_words, w_scales, b, dw, bn, out):
             grouped = regrouped.tile([P, ROWS * 4], BF16, align_bytes=64)
             grouped_tiles[g] = grouped
             nc.scalar.copy(
+                out=grouped[:].bitcast(F32).rearrange("p (c n u) -> p c n u", n=NB, u=2),
+                in_=xt_tiles[g][:].rearrange("p u (n c) -> p c n u", n=NB),
+            )
+
+        def regroup_x_v(g):
+            grouped = regrouped.tile([P, ROWS * 4], BF16, align_bytes=64)
+            grouped_tiles[g] = grouped
+            nc.vector.tensor_copy(
                 out=grouped[:].bitcast(F32).rearrange("p (c n u) -> p c n u", n=NB, u=2),
                 in_=xt_tiles[g][:].rearrange("p u (n c) -> p c n u", n=NB),
             )
@@ -254,7 +289,7 @@ def tile_timeception_pa_e_kernel(tc, x, w_words, w_scales, b, dw, bn, out):
 
         def multiply(j):
             v, pair = steps[j]
-            y = psum_y.tile([P, 2, ROWS], F32)
+            y = psum_y.tile([P, 2, ROWS], F32, tag="y")
             y_tiles[j] = y
             for i in range(2):
                 g = 2 * pair + i
@@ -288,13 +323,21 @@ def tile_timeception_pa_e_kernel(tc, x, w_words, w_scales, b, dw, bn, out):
                         func=ACT.Copy, scale=sign[:, g : g + 1],
                     )
                 return
-            if (v, pair // 2) == TURNED_CONV:
+            if (v, pair // 2) in TURNED:
+                half = v, pair // 2
+                pad = PAD[half]
                 for i in range(2):
-                    place = 2 * (pair % 2) + i
+                    g = 2 * pair + i
+                    if CENTRE[half] == "scalar":
+                        nc.scalar.activation(
+                            out=product[half][:, 1, g % HALF].rearrange("p two (m c) -> p two m c", c=STEP)[:, :, pad : pad + OUT_T, :],
+                            in_=y_tiles[j][:, i, :].rearrange("p (m two c) -> p two m c", two=2, c=STEP),
+                            func=ACT.Identity, bias=centre_offset[:, v, g : g + 1], scale=taps[:, v - 1, 1, g : g + 1],
+                        )
                     nc.scalar.activation(
-                        out=padded[:, place, :, PAD : PAD + OUT_T, :],
+                        out=padded[half][:, g % HALF, :, pad : pad + OUT_T, :],
                         in_=y_tiles[j][:, i, :].rearrange("p (m two c) -> p two m c", two=2, c=STEP),
-                        func=ACT.Identity, bias=own_bias[:, place : place + 1], scale=1.0,
+                        func=ACT.Identity, bias=own_bias[:, v, g : g + 1], scale=1.0,
                     )
                 return
             if v not in z_tiles:
@@ -377,12 +420,6 @@ def tile_timeception_pa_e_kernel(tc, x, w_words, w_scales, b, dw, bn, out):
                     scale=scale[:, v, g : g + 1], bias=offset[:, v, g : g + 1],
                 )
 
-        def finished(j):
-            if 0 <= j < len(steps) and steps[j][1] % 2 == 1:
-                half = steps[j][0], steps[j][1] // 2
-                return None if half == TURNED_CONV else half
-            return None
-
         def mend_edges(v, h):
             groups = slice(HALF * h, HALF * (h + 1))
             w = v * STEP
@@ -428,31 +465,51 @@ def tile_timeception_pa_e_kernel(tc, x, w_words, w_scales, b, dw, bn, out):
         parity_tiles = {}
         relu_tiles = {}
 
-        def convolve_turned(k):
-            i, parity = k // 2, k % 2
+        def convolve_turned(half, k):
+            v, h = half
+            parity, i = k // HALF, k % HALF
+            g = HALF * h + i
             if i == 0:
-                parity_tile = psum_t.tile([P, HALF, P], F32, tag="xt")
-                parity_tiles[parity] = parity_tile
-            target = parity_tiles[parity][:, i, :]
+                parity_tile = psum_x.tile([P, HALF, P], F32, tag="xt")
+                parity_tiles[half, parity] = parity_tile
+            target = parity_tiles[half, parity][:, i, :]
             for tap in range(3):
-                from_first = parity + (tap - 1) * turned_v
-                first = (PAD + from_first // 2) * STEP
-                source = padded[:, i, from_first % 2].rearrange("p m c -> p (m c)")
+                from_first = parity + (tap - 1) * v
+                first = (PAD[half] + from_first // 2) * STEP
+                if half in SCALED:
+                    nc.tensor.matmul(
+                        target, lhsT=product[half][:, tap, i, from_first % 2, first : first + COLS], rhs=ident[:],
+                        is_transpose=True, start=(tap == 0), stop=(tap == 2),
+                    )
+                else:
+                    source = padded[half][:, i, from_first % 2].rearrange("p m c -> p (m c)")
+                    nc.tensor.matmul(
+                        target, lhsT=source[:, first : first + COLS], rhs=diag[:, tap, i, :],
+                        start=(tap == 0), stop=False,
+                    )
+            if half not in SCALED:
                 nc.tensor.matmul(
-                    target, lhsT=source[:, first : first + COLS], rhs=diag[:, tap, i, :],
-                    start=(tap == 0), stop=False,
+                    target, lhsT=shift[:, v, g : g + 1].to_broadcast([P, P]), rhs=ident[:],
+                    is_transpose=True, start=False, stop=True,
                 )
-            nc.tensor.matmul(
-                target, lhsT=shift[:, i : i + 1].to_broadcast([P, P]), rhs=ident[:],
-                is_transpose=True, start=False, stop=True,
+
+        def relu_even(half):
+            relu = merged.tile([P, P, HALF], F32)
+            relu_tiles[half] = relu
+            nc.scalar.activation(
+                out=relu[:], in_=parity_tiles[half, 0][:].rearrange("p g o -> p o g"), func=ACT.Relu
             )
 
-        def relu_even():
-            relu = merged.tile([P, P, HALF], F32)
-            relu_tiles[0] = relu
-            nc.scalar.activation(
-                out=relu[:], in_=parity_tiles[0][:].rearrange("p g o -> p o g"), func=ACT.Relu
+        def merge_odd(half):
+            v, h = half
+            if v not in results:
+                result = outcome.tile([P, P, G], F32)
+                results[v] = result
+            nc.vector.tensor_max(
+                out=results[v][:, :, HALF * h : HALF * (h + 1)],
+                in0=parity_tiles[half, 1][:].rearrange("p g o -> p o g"), in1=relu_tiles[half][:],
             )
+            store_when_whole(v)
 
         halves_in = []
 
@@ -465,16 +522,6 @@ def tile_timeception_pa_e_kernel(tc, x, w_words, w_scales, b, dw, bn, out):
                         in_=results[v][n:P:NB].rearrange("p o g -> p (o g)"),
                     )
 
-        def merge_odd():
-            if turned_v not in results:
-                result = outcome.tile([P, P, G], F32)
-                results[turned_v] = result
-            nc.vector.tensor_max(
-                out=results[turned_v][:, :, turned_groups],
-                in0=parity_tiles[1][:].rearrange("p g o -> p o g"), in1=relu_tiles[0][:],
-            )
-            store_when_whole(turned_v)
-
         def shuffle_out(v, h):
             if v not in results:
                 result = outcome.tile([P, P, G], F32)
@@ -486,70 +533,184 @@ def tile_timeception_pa_e_kernel(tc, x, w_words, w_scales, b, dw, bn, out):
             )
             store_when_whole(v)
 
-        def is_tapped(j):
-            return steps[j][0] in CONV and (steps[j][0], steps[j][1] // 2) != TURNED_CONV
+        queues = {"tensor": [], "scalar": [], "vector": [], "gpsimd": []}
+        last_step = {}
+        for j in range(len(steps)):
+            last_step[steps[j][0], steps[j][1] // 2] = j
 
-        def turned_now(j):
-            found = []
-            for lag in (3, 2, 1):
-                half = finished(j - lag)
-                if half is not None and lag == {0: 1, 4: 2}.get(half[0], 3):
-                    found.append(half)
-            return found
+        def put(engine, makes, needs, call):
+            queues[engine].append((makes, needs, call))
+
+        def put_step(j, x):
+            pass
+
+        def t_x(g):
+            put("tensor", ("x", g), (), lambda: transpose_x(g))
+
+        def t_y(j):
+            pair = steps[j][1]
+            put("tensor", ("y", j), (("q", 2 * pair), ("q", 2 * pair + 1)), lambda: multiply(j))
+
+        def t_turn(half):
+            v, h = half
+            f = last_step[half]
+            if half in TURNED:
+                return
+            need = ("p", half)
+            if v == 4:
+                need = ("n", f)
+            if v == 0:
+                need = ("t", f)
+            put("tensor", ("u", half), (need,), lambda: turn(*half))
+
+        def t_piece(half, k):
+            put("tensor", ("e", half, k), tuple(("c", half, 3 * (k % HALF) + tap) for tap in range(3) if CENTRE[half] != "scalar" or tap != 1), lambda: convolve_turned(half, k))
+
+        def s_x(g):
+            put("scalar", ("r", g), (("x", g),), lambda: regroup_x(g))
+
+        def s_y(j):
+            put("scalar", ("z", j), (("y", j), ("const", 0)), lambda: leave_psum(j))
+
+        def s_norm(j):
+            put("scalar", ("n", j), (("t", j),), lambda: normalise(j))
+
+        def s_out(half):
+            if half in TURNED:
+                return
+            put("scalar", ("s", half), (("u", half),), lambda: shuffle_out(*half))
+
+        def s_relu(half):
+            put("scalar", ("h", half), tuple(("e", half, k) for k in range(HALF)), lambda: relu_even(half))
+
+        def v_x(g):
+            put("vector", ("q", g), (("r", g),), lambda: quantise_x(g))
+
+        def tapped(j):
+            return steps[j][0] in CONV and (steps[j][0], steps[j][1] // 2) not in TURNED
+
+        def v_first(j):
+            if tapped(j):
+                put("vector", ("t0", j), (("z", j),), lambda: add_tap(j, 0))
+            if steps[j][0] == 4:
+                put("vector", ("t0", j), (("z", j),), lambda: widen(j))
+
+        def v_second(j):
+            if tapped(j):
+                put("vector", ("t", j), (("t0", j),), lambda: add_tap(j, 2))
+            if steps[j][0] == 4:
+                put("vector", ("t", j), (("t0", j),), lambda: choose(j))
+            if steps[j][0] == 0:
+                put("vector", ("t", j), (("z", j),), lambda: pool_plain(j))
+
+        def v_pool(half):
+            put("vector", ("p", half), (("m", half),), lambda: pool_pairs(*half))
+
+        def v_merge(half):
+            put("vector", ("s", half), (("h", half),) + tuple(("e", half, k) for k in range(HALF, 2 * HALF)), lambda: merge_odd(half))
+
+        def g_mend(half):
+            f = last_step[half]
+            put("gpsimd", ("m", half), tuple(("t", j) for j in range(len(steps)) if (steps[j][0], steps[j][1] // 2) == half), lambda: mend_edges(*half))
+
+        def g_product(half, n):
+            v, h = half
+            j = steps.index((v, 2 * h + n // 6))
+            if CENTRE[half] == "scalar" and n % 3 == 1:
+                return
+            if CENTRE[half] == "vector" and n % 3 == 1:
+                put("vector", ("c", half, n), (("z", j),), lambda: scale_tap(half, n, nc.vector))
+                return
+            put("gpsimd", ("c", half, n), (("z", j),), lambda: scale_tap(half, n, nc.gpsimd))
+
+        put("tensor", ("x", 0), (), lambda: transpose_x(0))
+        put("tensor", ("par", 0), (), transpose_parameters)
+        put("scalar", ("r", 0), (("x", 0),), lambda: regroup_x(0))
+        put("scalar", ("inv", 0), (("par", 0),), invert_std)
+        put("vector", ("pre", 0), (("par", 0),), before_scale)
+        put("vector", ("q", 0), (("r", 0),), lambda: quantise_x(0))
+        put("vector", ("after", 0), (("inv", 0), ("pre", 0)), after_scale)
+        put("vector", ("q", 1), (("r", 1),), lambda: quantise_x(1))
+        put("vector", ("edge", 0), (("after", 0),), edge_terms)
+        put("vector", ("const", 0), (("edge", 0),), turned_constants)
+
+        def v_r(g):
+            put("vector", ("r", g), (("x", g),), lambda: regroup_x_v(g))
+
+        by_vector = ()
+        for g in (1, 2, 3):
+            t_x(g)
+            if g in by_vector:
+                v_r(g)
+            else:
+                s_x(g)
+        for g in (2, 3):
+            v_x(g)
+        n = len(steps)
+        for j in range(-1, n + 6):
+            if j + 1 < PAIRS - 1:
+                t_y(j + 1)
+                for g in (2 * j + 6, 2 * j + 7):
+                    if 4 <= g < G:
+                        t_x(g)
+            elif j + 1 == PAIRS - 1:
+                t_y(j + 1)
+                t_y(j + 2)
+            elif j + 2 < n:
+                t_y(j + 2)
+            for half in HALVES:
+                if last_step[half] + {0: 1, 4: 2}.get(half[0], 3) == j:
+                    t_turn(half)
+            for half, k in PIECES.get(j, ()):
+                t_piece(half, k)
+            if 0 <= j + 1 < n and True:
+                s_y(j + 1)
+            for g in (2 * j + 6, 2 * j + 7):
+                if 4 <= g < G and g not in by_vector:
+                    s_x(g)
+            if 0 <= j - 1 < n and steps[j - 1][0] == 4:
+                s_norm(j - 1)
+            for half in HALVES:
+                if half in TURNED:
+                    if RELU[half] == j:
+                        s_relu(half)
+                elif last_step[half] + {0: 1, 4: 2}.get(half[0], 3) + 1 == j:
+                    s_out(half)
+            if 0 <= j < n:
+                v_first(j)
+            for half in HALVES:
+                if half[0] in CONV and half not in TURNED:
+                    if last_step[half] + 1 == j:
+                        g_mend(half)
+                    if last_step[half] + 2 == j:
+                        v_pool(half)
+            if 0 <= j < n:
+                v_second(j)
+            for half in TURNED:
+                if MERGE[half] == j:
+                    v_merge(half)
+            for half, k in PRODUCTS.get(j, ()):
+                g_product(half, k)
+            for g in (2 * j + 6, 2 * j + 7):
+                if 4 <= g < G and g in by_vector:
+                    v_r(g)
+            for g in (2 * j + 4, 2 * j + 5):
+                if 4 <= g < G:
+                    v_x(g)
 
         with tc.manual_schedule():
-            transpose_x(0)
-            transpose_parameters()
-            transpose_x(1)
-            regroup_x(0)
-            invert_std()
-            regroup_x(1)
-            before_scale()
-            quantise_x(0)
-            after_scale()
-            quantise_x(1)
-            edge_terms()
-            turned_constants()
-            for j in range(-3, len(steps) + 5):
-                now = steps[j] if 0 <= j < len(steps) else None
-                if now is not None and is_tapped(j):
-                    add_tap(j, 0)
-                if now is not None and now[0] == 4:
-                    widen(j)
-                if finished(j - 1) is not None and finished(j - 1)[0] in CONV:
-                    mend_edges(*finished(j - 1))
-                if finished(j - 2) is not None and finished(j - 2)[0] in CONV:
-                    pool_pairs(*finished(j - 2))
-                if now is not None and is_tapped(j):
-                    add_tap(j, 2)
-                if now is not None and now[0] == 4:
-                    choose(j)
-                if now is not None and now[0] == 0:
-                    pool_plain(j)
-                if j == MERGE:
-                    merge_odd()
-                if 1 <= j + 2 < PAIRS:
-                    quantise_x(2 * (j + 2))
-                    quantise_x(2 * (j + 2) + 1)
-
-                if 0 <= j + 2 < len(steps):
-                    multiply(j + 2)
-                for half in turned_now(j):
-                    turn(*half)
-                if FIRST <= j < FIRST + 2 * HALF * STRIDE and (j - FIRST) % STRIDE == 0:
-                    convolve_turned((j - FIRST) // STRIDE)
-                if 1 <= j + 4 < PAIRS:
-                    transpose_x(2 * (j + 4))
-                    transpose_x(2 * (j + 4) + 1)
-
-                if 0 <= j + 1 < len(steps):
-                    leave_psum(j + 1)
-                if 1 <= j + 3 < PAIRS:
-                    regroup_x(2 * (j + 3))
-                    regroup_x(2 * (j + 3) + 1)
-                if 0 <= j - 1 < len(steps) and steps[j - 1][0] == 4:
-                    normalise(j - 1)
-                if j == MERGE - 1:
-                    relu_even()
-                for half in turned_now(j - 1):
-                    shuffle_out(*half)
+            written = set()
+            places = {engine: 0 for engine in queues}
+            left = sum(len(queues[engine]) for engine in queues)
+            while left > 0:
+                before = left
+                for engine in ("tensor", "scalar", "vector", "gpsimd"):
+                    place = places[engine]
+                    if place < len(queues[engine]):
+                        makes, needs, call = queues[engine][place]
+                        if all(need in written for need in needs):
+                            call()
+                            written.add(makes)
+                            places[engine] = place + 1
+                            left -= 1
+                assert left < before, str([(e, queues[e][places[e]][0:2]) for e in queues if places[e] < len(queues[e])])

@@ -29,15 +29,7 @@ COLS = OUT_T * STEP
 PAIRS = G // 2
 HALF = G // 2
 
-DIAGONAL = (9, 9)
-SCALED = ((3, 1), (1, 0),)
-TURNED = ((3, 1), (1, 0),)
-PIECES = {9: [((3, 1), 0), ((3, 1), 1), ((3, 1), 2), ((3, 1), 3)], 10: [((3, 1), 4), ((3, 1), 5), ((3, 1), 6), ((3, 1), 7)], 17: [((1, 0), 0), ((1, 0), 1), ((1, 0), 2), ((1, 0), 3)], 18: [((1, 0), 4), ((1, 0), 5), ((1, 0), 6), ((1, 0), 7)]}
-MERGE = {(3, 1): 12, (1, 0): 20}
-RELU = {(3, 1): 11, (1, 0): 19}
-CENTRE = {(3, 1): "vector", (1, 0): "vector"}
-PRODUCTS = {3: [((3, 1), 0), ((3, 1), 1), ((3, 1), 2)], 4: [((3, 1), 3), ((3, 1), 4), ((3, 1), 5)], 5: [((3, 1), 6), ((3, 1), 7), ((3, 1), 8)], 6: [((3, 1), 9), ((3, 1), 10), ((3, 1), 11)], 13: [((1, 0), 0), ((1, 0), 1), ((1, 0), 2)], 14: [((1, 0), 3), ((1, 0), 4), ((1, 0), 5)], 15: [((1, 0), 6), ((1, 0), 7), ((1, 0), 8)], 16: [((1, 0), 9), ((1, 0), 10), ((1, 0), 11)]}
-HALVES = tuple((v, h) for v in range(5) for h in range(2))
+TURNED = (3, 1)
 
 CONV = (3, 2, 1)
 
@@ -138,7 +130,7 @@ def tile_timeception_pa_e_kernel(tc, x, w_words, w_scales, b, dw, bn, out):
         beta = bn_par[:, :, 1, :]
         mean = bn_par[:, :, 2, :]
         var = bn_par[:, :, 3, :]
-        bias = par_ps[:, :, 32:40]
+        bias = keep.tile([P, NV, G], F32)
         dw_par = par_ps[:, 0:3, 64:88].rearrange("p i (j g) -> p i j g", j=3)
 
         inv_std = keep.tile([P, NV, G], F32)
@@ -159,80 +151,75 @@ def tile_timeception_pa_e_kernel(tc, x, w_words, w_scales, b, dw, bn, out):
                 out=inv_std[:], in_=var, func=ACT.Abs_reciprocal_sqrt, bias=EPS, scale=1.0
             )
 
-        def before_scale():
+        def copy_bias():
+            nc.scalar.copy(out=bias[:], in_=par_ps[:, :, 32:40])
+
+        def sum_taps():
             nc.vector.tensor_reduce(
                 out=tap_sum[:, 1:4, :], in_=dw_par.rearrange("p i j g -> p i g j"),
                 axis=mybir.AxisListType.X, op=ALU.add,
             )
-            nc.vector.tensor_mul(out=offset[:], in0=tap_sum[:], in1=bias)
-            nc.vector.tensor_sub(out=offset[:], in0=offset[:], in1=mean)
 
-        def after_scale():
+        def count_bias():
+            nc.vector.tensor_mul(out=offset[:], in0=tap_sum[:], in1=bias[:])
+
+        def scale_taps():
             nc.vector.tensor_mul(out=scale[:], in0=inv_std[:], in1=gamma)
+            nc.vector.tensor_sub(out=offset[:], in0=offset[:], in1=mean)
             nc.vector.tensor_mul(
                 out=taps[:], in0=dw_par, in1=scale[:, 1:4, :].unsqueeze(2).to_broadcast(spread)
             )
             nc.vector.tensor_mul(out=offset[:], in0=offset[:], in1=scale[:])
+
+        def finish_offset():
             nc.vector.tensor_add(out=offset[:], in0=offset[:], in1=beta)
 
         sign = keep.tile([P, G], F32)
         even = keep.tile([P, G, OUT_T + 1, STEP], F32)
 
-        def edge_terms():
+        def scale_bias():
             nc.vector.tensor_mul(
                 out=tap_bias[:], in0=taps[:], in1=bias[:, 1:4, :].unsqueeze(2).to_broadcast(spread)
             )
-            nc.vector.tensor_scalar(
-                out=sign[:], in0=scale[:, 4, :], scalar1=0.0, scalar2=2.0,
-                op0=ALU.is_ge, op1=ALU.mult,
-            )
-            nc.vector.tensor_scalar_add(out=sign[:], in0=sign[:], scalar1=-1.0)
-            nc.vector.tensor_scalar_mul(
-                out=even[:, :, OUT_T, :],
-                in0=sign[:].unsqueeze(2).to_broadcast([P, G, STEP]),
-                scalar1=-FAR,
-            )
 
-        PAD = {half: (half[0] + 1) // 2 for half in TURNED}
-        padded = {}
-        for half in TURNED:
-            pad = PAD[half]
-            tile = keep.tile([P, HALF, 2, OUT_T + 2 * pad, STEP], F32, name="padded%d%d" % half)
-            padded[half] = tile
-            nc.gpsimd.memset(tile[:, :, :, 0:pad, :], 0.0)
-            nc.gpsimd.memset(tile[:, :, :, pad + OUT_T :, :], 0.0)
-        diag = None
-        product = {}
-        for half in SCALED:
-            tile = keep.tile([P, 3, HALF, 2, (OUT_T + 2 * PAD[half]) * STEP], F32, name="product%d%d" % half)
-            product[half] = tile
-        own_bias = keep.tile([P, NV, G], F32)
-        shift = keep.tile([P, NV, G], F32)
-        centre_offset = keep.tile([P, NV, G], F32)
+        def make_sign(part):
+            if part == 0:
+                nc.vector.tensor_scalar(
+                    out=sign[:], in0=scale[:, 4, :], scalar1=0.0, scalar2=2.0,
+                    op0=ALU.is_ge, op1=ALU.mult,
+                )
+            if part == 1:
+                nc.vector.tensor_scalar_add(out=sign[:], in0=sign[:], scalar1=-1.0)
+            if part == 2:
+                nc.vector.tensor_scalar_mul(
+                    out=even[:, :, OUT_T, :],
+                    in0=sign[:].unsqueeze(2).to_broadcast([P, G, STEP]),
+                    scalar1=-FAR,
+                )
 
-        def turned_constants():
-            nc.vector.tensor_copy(out=own_bias[:], in_=bias)
-            nc.vector.tensor_mul(out=shift[:], in0=scale[:], in1=mean)
-            v, h = DIAGONAL
-            for i in range(HALF if DIAGONAL in TURNED else 0):
-                g = HALF * h + i
-                for tap in range(3):
+        turned_v, turned_h = TURNED
+        turned_groups = slice(HALF * turned_h, HALF * (turned_h + 1))
+        PAD = (turned_v + 1) // 2
+        padded = keep.tile([P, HALF, 2, OUT_T + 2 * PAD, STEP], F32)
+        diag = keep.tile([P, 3, HALF, P], F32)
+
+        def fill_padding(parity):
+            outside = [P, HALF, PAD * STEP]
+            minus = bias[:, turned_v, turned_groups].unsqueeze(2).to_broadcast(outside)
+            for first in (0, PAD + OUT_T):
+                nc.vector.tensor_scalar_mul(
+                    out=padded[:, :, parity, first : first + PAD, :].rearrange("p i m c -> p i (m c)"),
+                    in0=minus, scalar1=-1.0,
+                )
+
+        def make_diagonals():
+            for tap in range(3):
+                for i in range(HALF):
+                    g = HALF * turned_h + i
                     nc.gpsimd.tensor_scalar(
-                        out=diag[:, tap, i, :], in0=ident[:], scalar1=taps[:, v - 1, tap, g : g + 1],
+                        out=diag[:, tap, i, :], in0=ident[:], scalar1=taps[:, turned_v - 1, tap, g : g + 1],
                         scalar2=0.0, op0=ALU.mult, op1=ALU.add,
                     )
-            nc.vector.tensor_sub(out=shift[:], in0=beta, in1=shift[:])
-            nc.vector.tensor_add(out=centre_offset[:, 1:4, :], in0=shift[:, 1:4, :], in1=tap_bias[:, :, 1, :])
-
-        def scale_tap(half, n, engine):
-            v, h = half
-            i, tap = n // 3, n % 3
-            g = HALF * h + i
-            engine.tensor_scalar(
-                out=product[half][:, tap, i], in0=padded[half][:, i].rearrange("p two m c -> p two (m c)"),
-                scalar1=taps[:, v - 1, tap, g : g + 1],
-                scalar2=shift[:, v, g : g + 1] if tap == 1 else 0.0, op0=ALU.mult, op1=ALU.add,
-            )
 
         x_codes = keep.tile([P, G, ROWS], U32, align_bytes=64)
         x_planes = keep.tile([P, G, ROWS], U8, align_bytes=64)
@@ -323,21 +310,12 @@ def tile_timeception_pa_e_kernel(tc, x, w_words, w_scales, b, dw, bn, out):
                         func=ACT.Copy, scale=sign[:, g : g + 1],
                     )
                 return
-            if (v, pair // 2) in TURNED:
-                half = v, pair // 2
-                pad = PAD[half]
+            if (v, pair // 2) == TURNED:
                 for i in range(2):
-                    g = 2 * pair + i
-                    if CENTRE[half] == "scalar":
-                        nc.scalar.activation(
-                            out=product[half][:, 1, g % HALF].rearrange("p two (m c) -> p two m c", c=STEP)[:, :, pad : pad + OUT_T, :],
-                            in_=y_tiles[j][:, i, :].rearrange("p (m two c) -> p two m c", two=2, c=STEP),
-                            func=ACT.Identity, bias=centre_offset[:, v, g : g + 1], scale=taps[:, v - 1, 1, g : g + 1],
-                        )
-                    nc.scalar.activation(
-                        out=padded[half][:, g % HALF, :, pad : pad + OUT_T, :],
+                    place = 2 * (pair % 2) + i
+                    nc.scalar.copy(
+                        out=padded[:, place, :, PAD : PAD + OUT_T, :],
                         in_=y_tiles[j][:, i, :].rearrange("p (m two c) -> p two m c", two=2, c=STEP),
-                        func=ACT.Identity, bias=own_bias[:, v, g : g + 1], scale=1.0,
                     )
                 return
             if v not in z_tiles:
@@ -465,51 +443,41 @@ def tile_timeception_pa_e_kernel(tc, x, w_words, w_scales, b, dw, bn, out):
         parity_tiles = {}
         relu_tiles = {}
 
-        def convolve_turned(half, k):
-            v, h = half
-            parity, i = k // HALF, k % HALF
-            g = HALF * h + i
+        def convolve_turned(parity, i):
+            g = HALF * turned_h + i
             if i == 0:
                 parity_tile = psum_x.tile([P, HALF, P], F32, tag="xt")
-                parity_tiles[half, parity] = parity_tile
-            target = parity_tiles[half, parity][:, i, :]
+                parity_tiles[parity] = parity_tile
+            target = parity_tiles[parity][:, i, :]
             for tap in range(3):
-                from_first = parity + (tap - 1) * v
-                first = (PAD[half] + from_first // 2) * STEP
-                if half in SCALED:
-                    nc.tensor.matmul(
-                        target, lhsT=product[half][:, tap, i, from_first % 2, first : first + COLS], rhs=ident[:],
-                        is_transpose=True, start=(tap == 0), stop=(tap == 2),
-                    )
-                else:
-                    source = padded[half][:, i, from_first % 2].rearrange("p m c -> p (m c)")
-                    nc.tensor.matmul(
-                        target, lhsT=source[:, first : first + COLS], rhs=diag[:, tap, i, :],
-                        start=(tap == 0), stop=False,
-                    )
-            if half not in SCALED:
+                from_first = parity + (tap - 1) * turned_v
+                first = (PAD + from_first // 2) * STEP
+                source = padded[:, i, from_first % 2].rearrange("p m c -> p (m c)")
                 nc.tensor.matmul(
-                    target, lhsT=shift[:, v, g : g + 1].to_broadcast([P, P]), rhs=ident[:],
-                    is_transpose=True, start=False, stop=True,
+                    target, lhsT=source[:, first : first + COLS], rhs=diag[:, tap, i, :],
+                    start=(tap == 0), stop=False,
                 )
+            nc.tensor.matmul(
+                target, lhsT=offset[:, turned_v, g : g + 1].to_broadcast([P, P]), rhs=ident[:],
+                is_transpose=True, start=False, stop=True,
+            )
 
-        def relu_even(half):
+        def relu_even():
             relu = merged.tile([P, P, HALF], F32)
-            relu_tiles[half] = relu
+            relu_tiles[0] = relu
             nc.scalar.activation(
-                out=relu[:], in_=parity_tiles[half, 0][:].rearrange("p g o -> p o g"), func=ACT.Relu
+                out=relu[:], in_=parity_tiles[0][:].rearrange("p g o -> p o g"), func=ACT.Relu
             )
 
-        def merge_odd(half):
-            v, h = half
-            if v not in results:
+        def merge_odd():
+            if turned_v not in results:
                 result = outcome.tile([P, P, G], F32)
-                results[v] = result
+                results[turned_v] = result
             nc.vector.tensor_max(
-                out=results[v][:, :, HALF * h : HALF * (h + 1)],
-                in0=parity_tiles[half, 1][:].rearrange("p g o -> p o g"), in1=relu_tiles[half][:],
+                out=results[turned_v][:, :, turned_groups],
+                in0=parity_tiles[1][:].rearrange("p g o -> p o g"), in1=relu_tiles[0][:],
             )
-            store_when_whole(v)
+            store_when_whole(turned_v)
 
         halves_in = []
 
@@ -541,8 +509,9 @@ def tile_timeception_pa_e_kernel(tc, x, w_words, w_scales, b, dw, bn, out):
         def put(engine, makes, needs, call):
             queues[engine].append((makes, needs, call))
 
-        def put_step(j, x):
-            pass
+        def kind(j):
+            v, pair = steps[j]
+            return "turned" if (v, pair // 2) == TURNED else v
 
         def t_x(g):
             put("tensor", ("x", g), (), lambda: transpose_x(g))
@@ -552,106 +521,102 @@ def tile_timeception_pa_e_kernel(tc, x, w_words, w_scales, b, dw, bn, out):
             put("tensor", ("y", j), (("q", 2 * pair), ("q", 2 * pair + 1)), lambda: multiply(j))
 
         def t_turn(half):
-            v, h = half
             f = last_step[half]
-            if half in TURNED:
-                return
-            need = ("p", half)
-            if v == 4:
-                need = ("n", f)
-            if v == 0:
-                need = ("t", f)
+            need = {4: ("n", f), 0: ("t", f)}.get(half[0], ("p", half))
             put("tensor", ("u", half), (need,), lambda: turn(*half))
 
-        def t_piece(half, k):
-            put("tensor", ("e", half, k), tuple(("c", half, 3 * (k % HALF) + tap) for tap in range(3) if CENTRE[half] != "scalar" or tap != 1), lambda: convolve_turned(half, k))
+        def t_piece(parity, i):
+            j = steps.index((turned_v, 2 * turned_h + i // 2))
+            put("tensor", ("e", parity, i), (("z", j), ("diag", 0), ("fill", 0), ("fill", 1)), lambda: convolve_turned(parity, i))
 
         def s_x(g):
             put("scalar", ("r", g), (("x", g),), lambda: regroup_x(g))
 
         def s_y(j):
-            put("scalar", ("z", j), (("y", j), ("const", 0)), lambda: leave_psum(j))
+            need = {4: ("sign", 2)}.get(kind(j), ("after", 0))
+            put("scalar", ("z", j), (("y", j), need), lambda: leave_psum(j))
 
         def s_norm(j):
             put("scalar", ("n", j), (("t", j),), lambda: normalise(j))
 
         def s_out(half):
-            if half in TURNED:
-                return
             put("scalar", ("s", half), (("u", half),), lambda: shuffle_out(*half))
 
-        def s_relu(half):
-            put("scalar", ("h", half), tuple(("e", half, k) for k in range(HALF)), lambda: relu_even(half))
+        def s_relu():
+            put("scalar", ("h", 0), tuple(("e", 0, i) for i in range(HALF)), relu_even)
 
         def v_x(g):
             put("vector", ("q", g), (("r", g),), lambda: quantise_x(g))
 
-        def tapped(j):
-            return steps[j][0] in CONV and (steps[j][0], steps[j][1] // 2) not in TURNED
+        def v_r(g):
+            put("vector", ("r", g), (("x", g),), lambda: regroup_x_v(g))
 
         def v_first(j):
-            if tapped(j):
+            if kind(j) in CONV:
                 put("vector", ("t0", j), (("z", j),), lambda: add_tap(j, 0))
-            if steps[j][0] == 4:
+            if kind(j) == 4:
                 put("vector", ("t0", j), (("z", j),), lambda: widen(j))
 
         def v_second(j):
-            if tapped(j):
+            if kind(j) in CONV:
                 put("vector", ("t", j), (("t0", j),), lambda: add_tap(j, 2))
-            if steps[j][0] == 4:
+            if kind(j) == 4:
                 put("vector", ("t", j), (("t0", j),), lambda: choose(j))
-            if steps[j][0] == 0:
+            if kind(j) == 0:
                 put("vector", ("t", j), (("z", j),), lambda: pool_plain(j))
 
         def v_pool(half):
             put("vector", ("p", half), (("m", half),), lambda: pool_pairs(*half))
 
-        def v_merge(half):
-            put("vector", ("s", half), (("h", half),) + tuple(("e", half, k) for k in range(HALF, 2 * HALF)), lambda: merge_odd(half))
+        def v_merge():
+            put("vector", ("s", TURNED), (("h", 0),) + tuple(("e", 1, i) for i in range(HALF)), merge_odd)
 
-        def g_mend(half):
-            f = last_step[half]
-            put("gpsimd", ("m", half), tuple(("t", j) for j in range(len(steps)) if (steps[j][0], steps[j][1] // 2) == half), lambda: mend_edges(*half))
+        def g_mend(half, engine="gpsimd"):
+            pairs = [j for j in range(len(steps)) if (steps[j][0], steps[j][1] // 2) == half]
+            put(engine, ("m", half), tuple(("t", j) for j in pairs) + (("bias", 0),), lambda: mend_edges(*half))
 
-        def g_product(half, n):
-            v, h = half
-            j = steps.index((v, 2 * h + n // 6))
-            if CENTRE[half] == "scalar" and n % 3 == 1:
-                return
-            if CENTRE[half] == "vector" and n % 3 == 1:
-                put("vector", ("c", half, n), (("z", j),), lambda: scale_tap(half, n, nc.vector))
-                return
-            put("gpsimd", ("c", half, n), (("z", j),), lambda: scale_tap(half, n, nc.gpsimd))
-
-        put("tensor", ("x", 0), (), lambda: transpose_x(0))
-        put("tensor", ("par", 0), (), transpose_parameters)
-        put("scalar", ("r", 0), (("x", 0),), lambda: regroup_x(0))
-        put("scalar", ("inv", 0), (("par", 0),), invert_std)
-        put("vector", ("pre", 0), (("par", 0),), before_scale)
-        put("vector", ("q", 0), (("r", 0),), lambda: quantise_x(0))
-        put("vector", ("after", 0), (("inv", 0), ("pre", 0)), after_scale)
-        put("vector", ("q", 1), (("r", 1),), lambda: quantise_x(1))
-        put("vector", ("edge", 0), (("after", 0),), edge_terms)
-        put("vector", ("const", 0), (("edge", 0),), turned_constants)
-
-        def v_r(g):
-            put("vector", ("r", g), (("x", g),), lambda: regroup_x_v(g))
+        HALVES = [(v, h) for v in range(NV) for h in range(2)]
+        TAPPED = [half for half in HALVES if half[0] in CONV and half != TURNED]
 
         by_vector = ()
+        t_x(0)
+        put("tensor", ("par", 0), (), transpose_parameters)
         for g in (1, 2, 3):
             t_x(g)
+        s_x(0)
+        put("scalar", ("inv", 0), (("par", 0),), invert_std)
+        put("scalar", ("copied", 0), (("par", 0),), copy_bias)
+        for g in (1, 2, 3):
             if g in by_vector:
-                v_r(g)
+                pass
             else:
                 s_x(g)
-        for g in (2, 3):
-            v_x(g)
+        put("vector", ("sum", 0), (("par", 0),), sum_taps)
+        put("vector", ("count", 0), (("sum", 0), ("copied", 0)), count_bias)
+        v_x(0)
+        put("vector", ("scale", 0), (("inv", 0), ("count", 0)), scale_taps)
+        v_x(1)
+        put("vector", ("after", 0), (("scale", 0),), finish_offset)
+        put("gpsimd", ("diag", 0), (("scale", 0),), make_diagonals)
+        for g in (1, 2, 3):
+            if g in by_vector:
+                v_r(g)
+        v_x(2)
+        v_x(3)
+
+        def v_small(name, part):
+            call = {"bias": scale_bias, "fill": lambda: fill_padding(part), "sign": lambda: make_sign(part)}[name]
+            need = ("copied", 0) if name == "fill" else ("after", 0)
+            put("vector", (name, part), (need,), call)
+
+        small = [("bias", 0), ("sign", 0), ("fill", 0), ("sign", 1), ("fill", 1), ("sign", 2)]
         n = len(steps)
+        steps_last = max(TAPPED, key=lambda half: last_step[half])
         for j in range(-1, n + 6):
             if j + 1 < PAIRS - 1:
                 t_y(j + 1)
                 for g in (2 * j + 6, 2 * j + 7):
-                    if 4 <= g < G:
+                    if g < G:
                         t_x(g)
             elif j + 1 == PAIRS - 1:
                 t_y(j + 1)
@@ -659,38 +624,45 @@ def tile_timeception_pa_e_kernel(tc, x, w_words, w_scales, b, dw, bn, out):
             elif j + 2 < n:
                 t_y(j + 2)
             for half in HALVES:
-                if last_step[half] + {0: 1, 4: 2}.get(half[0], 3) == j:
+                if half != TURNED and last_step[half] + {0: 1, 4: 2}.get(half[0], 4) == j:
                     t_turn(half)
-            for half, k in PIECES.get(j, ()):
-                t_piece(half, k)
-            if 0 <= j + 1 < n and True:
+            for k in range(2 * HALF):
+                if ([5,6,8,9,11,12,14,15])[k] == j:
+                    t_piece(k // HALF, k % HALF)
+            if 0 <= j + 1 < n:
                 s_y(j + 1)
             for g in (2 * j + 6, 2 * j + 7):
                 if 4 <= g < G and g not in by_vector:
                     s_x(g)
             if 0 <= j - 1 < n and steps[j - 1][0] == 4:
                 s_norm(j - 1)
+            if j == 12:
+                s_relu()
             for half in HALVES:
-                if half in TURNED:
-                    if RELU[half] == j:
-                        s_relu(half)
-                elif last_step[half] + {0: 1, 4: 2}.get(half[0], 3) + 1 == j:
+                if half != TURNED and last_step[half] + {0: 1, 4: 2}.get(half[0], 4) + 1 == j:
                     s_out(half)
-            if 0 <= j < n:
+            if 0 <= j < n and kind(j) != 4:
                 v_first(j)
-            for half in HALVES:
-                if half[0] in CONV and half not in TURNED:
-                    if last_step[half] + 1 == j:
-                        g_mend(half)
-                    if last_step[half] + 2 == j:
-                        v_pool(half)
+            if j + 1 < n and kind(j + 1) == 4 and j >= 0:
+                v_first(j + 1)
+            for half in TAPPED:
+                if last_step[half] + 1 == j:
+                    g_mend(half)
+                if last_step[half] + 2 == j and False:
+                    v_pool(half)
+            if j >= 0 and small:
+                v_small(*small[0])
+                small = small[1:]
             if 0 <= j < n:
                 v_second(j)
-            for half in TURNED:
-                if MERGE[half] == j:
-                    v_merge(half)
-            for half, k in PRODUCTS.get(j, ()):
-                g_product(half, k)
+            if j >= 0 and small:
+                v_small(*small[0])
+                small = small[1:]
+            for half in TAPPED:
+                if last_step[half] + 2 == j and True:
+                    v_pool(half)
+            if j == 18:
+                v_merge()
             for g in (2 * j + 6, 2 * j + 7):
                 if 4 <= g < G and g in by_vector:
                     v_r(g)

@@ -37,10 +37,9 @@ FLOPS = 2 * ROWS * K * P * NV * G
 
 
 def work_order():
-    steps = [(3, pair) for pair in range(PAIRS)]
-    for first, second in ((4, 2), (1, 0)):
-        for pair in range(PAIRS):
-            steps += [(first, pair), (second, pair)]
+    steps = [(3, 0), (3, 1), (3, 2), (4, 0), (3, 3), (2, 0), (4, 1), (2, 1), (4, 2), (2, 2), (4, 3), (2, 3)]
+    for pair in range(PAIRS):
+        steps += [(1, pair), (0, pair)]
     return steps
 
 
@@ -609,7 +608,7 @@ def tile_timeception_pa_e_kernel(tc, x, w_words, w_scales, b, dw, bn, out):
             need = ("copied", 0) if name == "fill" else ("after", 0)
             put("vector", (name, part), (need,), call)
 
-        small = [("bias", 0), ("sign", 0), ("fill", 0), ("sign", 1), ("fill", 1), ("sign", 2)]
+        small = [("sign", 0), ("sign", 1), ("sign", 2), ("bias", 0), ("fill", 0), ("fill", 1)]
         n = len(steps)
         steps_last = max(TAPPED, key=lambda half: last_step[half])
         for j in range(-1, n + 6):
@@ -627,7 +626,7 @@ def tile_timeception_pa_e_kernel(tc, x, w_words, w_scales, b, dw, bn, out):
                 if half != TURNED and last_step[half] + {0: 1, 4: 2}.get(half[0], 4) == j:
                     t_turn(half)
             for k in range(2 * HALF):
-                if ([5,6,8,9,11,12,14,15])[k] == j:
+                if ([6,7,9,10,12,13,15,16])[k] == j:
                     t_piece(k // HALF, k % HALF)
             if 0 <= j + 1 < n:
                 s_y(j + 1)
@@ -636,7 +635,7 @@ def tile_timeception_pa_e_kernel(tc, x, w_words, w_scales, b, dw, bn, out):
                     s_x(g)
             if 0 <= j - 1 < n and steps[j - 1][0] == 4:
                 s_norm(j - 1)
-            if j == 12:
+            if j == 11:
                 s_relu()
             for half in HALVES:
                 if half != TURNED and last_step[half] + {0: 1, 4: 2}.get(half[0], 4) + 1 == j:

@@ -37,7 +37,7 @@ FLOPS = 2 * ROWS * K * P * NV * G
 
 
 def work_order():
-    steps = [(3, 0), (3, 1), (3, 2), (4, 0), (3, 3), (2, 0), (4, 1), (2, 1), (4, 2), (2, 2), (4, 3), (2, 3)]
+    steps = [(3, 0), (3, 1), (3, 2), (4, 0), (3, 3), (4, 1), (2, 0), (2, 1), (4, 2), (2, 2), (4, 3), (2, 3)]
     for pair in range(PAIRS):
         steps += [(1, pair), (0, pair)]
     return steps
@@ -108,14 +108,16 @@ def tile_timeception_pa_e_kernel(tc, x, w_words, w_scales, b, dw, bn, out):
         load_parameters()
         load_x(1, 1)
         load_x(2, 3)
-        load_scales(3, 4)
+        load_scales(3, 3)
         load_words(3 * G, 3 * G + 2)
         load_x(4, 5)
         load_words(3 * G + 2, 4 * G)
         load_x(6, 7)
-        load_scales(0, 2)
+        load_scales(4, 4)
         load_words(4 * G, 5 * G)
+        load_scales(2, 2)
         load_words(2 * G, 3 * G)
+        load_scales(0, 1)
         load_words(0, 2 * G)
 
         ident_bf = keep.tile([P, P], BF16)

from contextlib import ExitStack

import concourse.mybir as mybir
from concourse.masks import make_identity

F32 = mybir.dt.float32
BF16 = mybir.dt.bfloat16
I32 = mybir.dt.int32
U32 = mybir.dt.uint32
U8 = mybir.dt.uint8
FP8X4 = mybir.dt.float8_e4m3fn_x4
FP4X4 = mybir.dt.float4_e2m1fn_x4
ALU = mybir.AluOpType
ACT = mybir.ActivationFunctionType

P = 128
NB = 2
T = 32
S = 4
G = 8
K = 512
NV = 5
EPS = 1e-3
FAR = 3.0e38
ROWS = NB * T * S
STEP = S * NB
OUT_T = T // 2
COLS = OUT_T * STEP
PAIRS = G // 2
HALF = G // 2

TURNED = (3, 1)

CONV = (3, 2, 1)

FLOPS = 2 * ROWS * K * P * NV * G


def work_order():
    steps = [(3, 0), (3, 1), (3, 2), (4, 0), (3, 3), (4, 1), (2, 0), (2, 1), (4, 2), (2, 2), (4, 3), (2, 3)]
    for pair in range(PAIRS):
        steps += [(1, pair), (0, pair)]
    return steps


def tile_timeception_pa_e_kernel(tc, x, w_words, w_scales, b, dw, bn, out):
    nc = tc.nc
    with ExitStack() as ctx:
        keep = ctx.enter_context(tc.tile_pool(name="keep", bufs=1))
        stage = ctx.enter_context(tc.tile_pool(name="stage", bufs=2))
        branch = ctx.enter_context(tc.tile_pool(name="branch", bufs=3))
        outcome = ctx.enter_context(tc.tile_pool(name="outcome", bufs=NV))
        regrouped = ctx.enter_context(tc.tile_pool(name="regrouped", bufs=4))
        fourth = ctx.enter_context(tc.tile_pool(name="fourth", bufs=2))
        merged = ctx.enter_context(tc.tile_pool(name="merged", bufs=2))
        psum_x = ctx.enter_context(tc.psum_pool(name="psum_x", bufs=2))
        psum_y = ctx.enter_context(tc.psum_pool(name="psum_y", bufs=4))
        psum_o = ctx.enter_context(tc.psum_pool(name="psum_o", bufs=2))

        one = keep.tile([P, 1], F32)
        nc.vector.memset(one[:], 1.0)
        rows = keep.tile([P, NV, P], BF16)
        nc.vector.memset(rows[:].bitcast(I32), 0)

        def load_parameters():
            nc.sync.dma_start(out=rows[0:32], in_=bn.rearrange("v j g o -> (j g) v o"))
            nc.sync.dma_start(out=rows[32:40], in_=b.rearrange("v g o -> g v o"))
            dw_rows = dw.rearrange("i j g o -> (j g) i o")
            nc.sync.dma_start(out=rows[64:80, 0:3, :], in_=dw_rows[0:16])
            nc.sync.dma_start(out=rows[80:88, 0:3, :], in_=dw_rows[16:24])

        nc.scalar.activation(out=one[:], in_=one[:], func=ACT.Abs_reciprocal_sqrt)

        w_planes = keep.tile([P, NV * G, P], U8, align_bytes=64)
        nc.vector.memset(w_planes[:].bitcast(I32), 0)
        w_sb = keep.tile([P, NV * G, 2 * P], U8, align_bytes=64)
        words_dram = w_words.bitcast(I32)
        scales_dram = w_scales.bitcast(I32)

        def load_scales(first_branch, last_branch):
            mats = slice(G * first_branch, G * (last_branch + 1))
            for r in range(4):
                nc.sync.dma_start(
                    out=w_planes[r:P:32, mats, :].bitcast(I32),
                    in_=scales_dram[mats, r:16:4, :].rearrange("e q c -> q e c"),
                )

        def load_words(first, last):
            mats = slice(first, last)
            nc.sync.dma_start(
                out=w_sb[:, mats, :].bitcast(I32),
                in_=words_dram[mats].rearrange("e p c -> p e c"),
            )

        x_rows = x.rearrange("n t p q c -> (t p q) n c")
        x_sb = {}

        def load_x(first_group, last_group):
            count = last_group + 1 - first_group
            piece = keep.tile([P, NB, K * count], BF16, name="x_sb%d" % first_group)
            nc.sync.dma_start(
                out=piece[:], in_=x_rows[:, :, K * first_group : K * (last_group + 1)]
            )
            for g in range(first_group, last_group + 1):
                x_sb[g] = (piece, g - first_group)

        load_x(0, 0)
        load_parameters()
        load_x(1, 1)
        load_x(2, 3)
        load_scales(3, 3)
        load_words(3 * G, 3 * G + 2)
        load_x(4, 5)
        load_words(3 * G + 2, 4 * G)
        load_x(6, 7)
        load_scales(4, 4)
        load_words(4 * G, 5 * G)
        load_scales(2, 2)
        load_words(2 * G, 3 * G)
        load_scales(0, 1)
        load_words(0, 2 * G)

        ident_bf = keep.tile([P, P], BF16)
        make_identity(nc, ident_bf[:])
        ident = keep.tile([P, P], F32)
        make_identity(nc, ident[:])

        par_ps = psum_y.tile([P, NV, P], BF16, tag="y")
        bn_par = par_ps[:, :, 0:32].rearrange("p v (j g) -> p v j g", j=4)
        gamma = bn_par[:, :, 0, :]
        beta = bn_par[:, :, 1, :]
        mean = bn_par[:, :, 2, :]
        var = bn_par[:, :, 3, :]
        bias = keep.tile([P, NV, G], F32)
        dw_par = par_ps[:, 0:3, 64:88].rearrange("p i (j g) -> p i j g", j=3)

        inv_std = keep.tile([P, NV, G], F32)
        tap_sum = keep.tile([P, NV, G], F32)
        nc.vector.memset(tap_sum[:], 1.0)
        offset = keep.tile([P, NV, G], F32)
        scale = keep.tile([P, NV, G], F32)
        spread = [P, 3, 3, G]
        taps = keep.tile(spread, F32)
        tap_bias = keep.tile(spread, F32)

        def transpose_parameters():
            for c in range(NV):
                nc.tensor.transpose(par_ps[:, c, :], rows[:, c, :], ident_bf[:])

        def invert_std():
            nc.scalar.activation(
                out=inv_std[:], in_=var, func=ACT.Abs_reciprocal_sqrt, bias=EPS, scale=1.0
            )

        def copy_bias():
            nc.scalar.copy(out=bias[:], in_=par_ps[:, :, 32:40])

        def sum_taps():
            nc.vector.tensor_reduce(
                out=tap_sum[:, 1:4, :], in_=dw_par.rearrange("p i j g -> p i g j"),
                axis=mybir.AxisListType.X, op=ALU.add,
            )

        def count_bias():
            nc.vector.tensor_mul(out=offset[:], in0=tap_sum[:], in1=bias[:])

        def scale_taps():
            nc.vector.tensor_mul(out=scale[:], in0=inv_std[:], in1=gamma)
            nc.vector.tensor_sub(out=offset[:], in0=offset[:], in1=mean)
            nc.vector.tensor_mul(
                out=taps[:], in0=dw_par, in1=scale[:, 1:4, :].unsqueeze(2).to_broadcast(spread)
            )
            nc.vector.tensor_mul(out=offset[:], in0=offset[:], in1=scale[:])

        def finish_offset():
            nc.vector.tensor_add(out=offset[:], in0=offset[:], in1=beta)

        sign = keep.tile([P, G], F32)
        even = keep.tile([P, G, OUT_T + 1, STEP], F32)

        def scale_bias():
            nc.vector.tensor_mul(
                out=tap_bias[:], in0=taps[:], in1=bias[:, 1:4, :].unsqueeze(2).to_broadcast(spread)
            )

        def make_sign(part):
            if part == 0:
                nc.vector.tensor_scalar(
                    out=sign[:], in0=scale[:, 4, :], scalar1=0.0, scalar2=2.0,
                    op0=ALU.is_ge, op1=ALU.mult,
                )
            if part == 1:
                nc.vector.tensor_scalar_add(out=sign[:], in0=sign[:], scalar1=-1.0)
            if part == 2:
                nc.vector.tensor_scalar_mul(
                    out=even[:, :, OUT_T, :],
                    in0=sign[:].unsqueeze(2).to_broadcast([P, G, STEP]),
                    scalar1=-FAR,
                )

        turned_v, turned_h = TURNED
        turned_groups = slice(HALF * turned_h, HALF * (turned_h + 1))
        PAD = (turned_v + 1) // 2
        padded = keep.tile([P, HALF, 2, OUT_T + 2 * PAD, STEP], F32)
        diag = keep.tile([P, 3, HALF, P], F32)

        def fill_padding(parity):
            outside = [P, HALF, PAD * STEP]
            minus = bias[:, turned_v, turned_groups].unsqueeze(2).to_broadcast(outside)
            for first in (0, PAD + OUT_T):
                nc.vector.tensor_scalar_mul(
                    out=padded[:, :, parity, first : first + PAD, :].rearrange("p i m c -> p i (m c)"),
                    in0=minus, scalar1=-1.0,
                )

        def make_diagonals():
            for tap in range(3):
                for i in range(HALF):
                    g = HALF * turned_h + i
                    nc.gpsimd.tensor_scalar(
                        out=diag[:, tap, i, :], in0=ident[:], scalar1=taps[:, turned_v - 1, tap, g : g + 1],
                        scalar2=0.0, op0=ALU.mult, op1=ALU.add,
                    )

        x_codes = keep.tile([P, G, ROWS], U32, align_bytes=64)
        x_planes = keep.tile([P, G, ROWS], U8, align_bytes=64)
        xt_tiles = {}
        grouped_tiles = {}

        def transpose_x(g):
            if g % 4 < 2:
                xt = psum_x.tile([P, 2, ROWS], F32, tag="xt")
            else:
                xt = psum_o.tile([P, 2, ROWS], F32, tag="turned")
            xt_tiles[g] = xt
            piece, place = x_sb[g]
            for n in range(NB):
                words = piece[:, n, :].bitcast(F32)
                for u in range(2):
                    nc.tensor.transpose(
                        xt[:, u, P * n : P * (n + 1)],
                        words[:, (K // 2) * place + u : (K // 2) * (place + 1) : 2],
                        ident[:],
                    )

        def regroup_x(g):
            grouped = regrouped.tile([P, ROWS * 4], BF16, align_bytes=64)
            grouped_tiles[g] = grouped
            nc.scalar.copy(
                out=grouped[:].bitcast(F32).rearrange("p (c n u) -> p c n u", n=NB, u=2),
                in_=xt_tiles[g][:].rearrange("p u (n c) -> p c n u", n=NB),
            )

        def regroup_x_v(g):
            grouped = regrouped.tile([P, ROWS * 4], BF16, align_bytes=64)
            grouped_tiles[g] = grouped
            nc.vector.tensor_copy(
                out=grouped[:].bitcast(F32).rearrange("p (c n u) -> p c n u", n=NB, u=2),
                in_=xt_tiles[g][:].rearrange("p u (n c) -> p c n u", n=NB),
            )

        def quantise_x(g):
            nc.vector.quantize_mx(
                out=x_codes[:, g, :].bitcast(FP8X4), scales=x_planes[:, g, :],
                in_=grouped_tiles[g][:],
            )

        steps = work_order()
        y_tiles = {}
        z_tiles = {}
        results = {}
        pooled_tiles = {}
        turned_tiles = {}

        def by_parity(ap, odd):
            return ap.rearrange("p (m two c) -> p m two c", two=2, c=STEP)[:, :, odd, :]

        def multiply(j):
            v, pair = steps[j]
            y = psum_y.tile([P, 2, ROWS], F32, tag="y")
            y_tiles[j] = y
            for i in range(2):
                g = 2 * pair + i
                nc.tensor.matmul_mx(
                    out=y[:, i, :],
                    lhsT=w_sb[:, G * v + g, :].bitcast(FP4X4),
                    lhsT_scale=w_planes[:, G * v + g, :],
                    rhs=x_codes[:, g, :].bitcast(FP8X4),
                    rhs_scale=x_planes[:, g, :],
                    start=True,
                    stop=True,
                )

        def leave_psum(j):
            v, pair = steps[j]
            if v == 0:
                scaled = fourth.tile([P, 2, OUT_T, STEP], F32)
                scaled_tiles[j] = scaled
                for i in range(2):
                    g = 2 * pair + i
                    nc.scalar.activation(
                        out=scaled[:, i], in_=by_parity(y_tiles[j][:, i, :], 0),
                        func=ACT.Copy, scale=scale[:, v, g : g + 1],
                    )
                return
            if v == 4:
                for i in range(2):
                    g = 2 * pair + i
                    nc.scalar.activation(
                        out=even[:, g, 0:OUT_T, :], in_=by_parity(y_tiles[j][:, i, :], 0),
                        func=ACT.Copy, scale=sign[:, g : g + 1],
                    )
                return
            if (v, pair // 2) == TURNED:
                for i in range(2):
                    place = 2 * (pair % 2) + i
                    nc.scalar.copy(
                        out=padded[:, place, :, PAD : PAD + OUT_T, :],
                        in_=y_tiles[j][:, i, :].rearrange("p (m two c) -> p two m c", two=2, c=STEP),
                    )
                return
            if v not in z_tiles:
                z = branch.tile([P, G, ROWS], F32)
                z_tiles[v] = z
            for i in range(2):
                g = 2 * pair + i
                zg = z_tiles[v][:, g, :]
                yg = y_tiles[j][:, i, :]
                nc.scalar.activation(
                    out=zg, in_=yg, func=ACT.Identity,
                    scale=taps[:, v - 1, 1, g : g + 1], bias=offset[:, v, g : g + 1],
                )

        def add_tap(j, tap):
            v, pair = steps[j]
            w = v * STEP
            for i in range(2):
                g = 2 * pair + i
                if tap == 0:
                    target, source = z_tiles[v][:, g, w:], y_tiles[j][:, i, : ROWS - w]
                else:
                    target, source = z_tiles[v][:, g, : ROWS - w], y_tiles[j][:, i, w:]
                nc.vector.scalar_tensor_tensor(
                    out=target, in0=source, scalar=taps[:, v - 1, tap, g : g + 1], in1=target,
                    op0=ALU.mult, op1=ALU.add,
                )

        window_tiles = {}
        scaled_tiles = {}

        def pool_plain(j):
            v, pair = steps[j]
            if pair % 2 == 0:
                chosen = fourth.tile([P, HALF, COLS], F32)
                pooled_tiles[v, pair // 2] = chosen
            for i in range(2):
                g = 2 * pair + i
                nc.vector.scalar_tensor_tensor(
                    out=pooled_tiles[v, pair // 2][:, g % HALF, :].rearrange(
                        "p (m c) -> p m c", c=STEP
                    ),
                    in0=by_parity(y_tiles[j][:, i, :], 1), scalar=scale[:, v, g : g + 1],
                    in1=scaled_tiles[j][:, i],
                    op0=ALU.mult, op1=ALU.max,
                )

        def widen(j):
            v, pair = steps[j]
            window = fourth.tile([P, 2, OUT_T, STEP], F32)
            window_tiles[j] = window
            for i in range(2):
                g = 2 * pair + i
                nc.vector.tensor_max(
                    out=window[:, i], in0=even[:, g, 0:OUT_T, :], in1=even[:, g, 1 : OUT_T + 1, :]
                )

        def choose(j):
            v, pair = steps[j]
            if pair % 2 == 0:
                chosen = fourth.tile([P, HALF, COLS], F32)
                pooled_tiles[v, pair // 2] = chosen
            for i in range(2):
                g = 2 * pair + i
                nc.vector.scalar_tensor_tensor(
                    out=pooled_tiles[v, pair // 2][:, g % HALF, :].rearrange(
                        "p (m c) -> p m c", c=STEP
                    ),
                    in0=window_tiles[j][:, i], scalar=sign[:, g : g + 1],
                    in1=by_parity(y_tiles[j][:, i, :], 1),
                    op0=ALU.mult, op1=ALU.max,
                )

        def normalise(j):
            v, pair = steps[j]
            for g in (2 * pair, 2 * pair + 1):
                chosen_g = pooled_tiles[v, pair // 2][:, g % HALF, :]
                nc.scalar.activation(
                    out=chosen_g, in_=chosen_g, func=ACT.Relu,
                    scale=scale[:, v, g : g + 1], bias=offset[:, v, g : g + 1],
                )

        def mend_edges(v, h):
            groups = slice(HALF * h, HALF * (h + 1))
            w = v * STEP
            for tap, cols in ((0, slice(0, w)), (2, slice(ROWS - w, ROWS))):
                extra = tap_bias[:, v - 1, tap, groups].unsqueeze(2)
                nc.gpsimd.tensor_tensor(
                    out=z_tiles[v][:, groups, cols],
                    in0=z_tiles[v][:, groups, cols],
                    in1=extra.to_broadcast([P, HALF, w]),
                    op=ALU.subtract,
                )

        def pool_pairs(v, h):
            groups = slice(HALF * h, HALF * (h + 1))
            pairs = z_tiles[v][:, groups, :].rearrange("p g (m two c) -> p (g m) two c", two=2, c=STEP)
            pooled = stage.tile([P, HALF, COLS], F32)
            pooled_tiles[v, h] = pooled
            nc.vector.scalar_tensor_tensor(
                out=pooled[:].rearrange("p g (m c) -> p (g m) c", c=STEP),
                in0=pairs[:, :, 0, :], scalar=0.0, in1=pairs[:, :, 1, :],
                op0=ALU.max, op1=ALU.max,
            )

        def turn(v, h):
            turned = psum_o.tile([P, HALF, P], F32, tag="turned")
            turned_tiles[v, h] = turned
            for i in range(HALF):
                if v == 0:
                    g = HALF * h + i
                    nc.tensor.matmul(
                        turned[:, i, :], lhsT=pooled_tiles[v, h][:, i, :], rhs=ident[:],
                        is_transpose=True, start=True, stop=False,
                    )
                    nc.tensor.matmul(
                        turned[:, i, :], lhsT=offset[:, v, g : g + 1].to_broadcast([P, P]), rhs=ident[:],
                        is_transpose=True, start=False, stop=True,
                    )
                else:
                    nc.tensor.transpose(turned[:, i, :], pooled_tiles[v, h][:, i, :], ident[:])

        out_rows = out.rearrange("n t p q c -> n (t p q) c")

        parity_tiles = {}
        relu_tiles = {}

        def convolve_turned(parity, i):
            g = HALF * turned_h + i
            if i == 0:
                parity_tile = psum_x.tile([P, HALF, P], F32, tag="xt")
                parity_tiles[parity] = parity_tile
            target = parity_tiles[parity][:, i, :]
            for tap in range(3):
                from_first = parity + (tap - 1) * turned_v
                first = (PAD + from_first // 2) * STEP
                source = padded[:, i, from_first % 2].rearrange("p m c -> p (m c)")
                nc.tensor.matmul(
                    target, lhsT=source[:, first : first + COLS], rhs=diag[:, tap, i, :],
                    start=(tap == 0), stop=False,
                )
            nc.tensor.matmul(
                target, lhsT=offset[:, turned_v, g : g + 1].to_broadcast([P, P]), rhs=ident[:],
                is_transpose=True, start=False, stop=True,
            )

        def relu_even():
            relu = merged.tile([P, P, HALF], F32)
            relu_tiles[0] = relu
            nc.scalar.activation(
                out=relu[:], in_=parity_tiles[0][:].rearrange("p g o -> p o g"), func=ACT.Relu
            )

        def merge_odd():
            if turned_v not in results:
                result = outcome.tile([P, P, G], F32)
                results[turned_v] = result
            nc.vector.tensor_max(
                out=results[turned_v][:, :, turned_groups],
                in0=parity_tiles[1][:].rearrange("p g o -> p o g"), in1=relu_tiles[0][:],
            )
            store_when_whole(turned_v)

        halves_in = []

        def store_when_whole(v):
            halves_in.append(v)
            if halves_in.count(v) == 2:
                for n in range(NB):
                    nc.sync.dma_start(
                        out=out_rows[n, :, P * G * v : P * G * (v + 1)],
                        in_=results[v][n:P:NB].rearrange("p o g -> p (o g)"),
                    )

        def shuffle_out(v, h):
            if v not in results:
                result = outcome.tile([P, P, G], F32)
                results[v] = result
            nc.scalar.activation(
                out=results[v][:, :, HALF * h : HALF * (h + 1)],
                in_=turned_tiles[v, h][:].rearrange("p g o -> p o g"),
                func=ACT.Relu,
            )
            store_when_whole(v)

        queues = {"tensor": [], "scalar": [], "vector": [], "gpsimd": []}
        last_step = {}
        for j in range(len(steps)):
            last_step[steps[j][0], steps[j][1] // 2] = j

        def put(engine, makes, needs, call):
            queues[engine].append((makes, needs, call))

        def kind(j):
            v, pair = steps[j]
            return "turned" if (v, pair // 2) == TURNED else v

        def t_x(g):
            put("tensor", ("x", g), (), lambda: transpose_x(g))

        def t_y(j):
            pair = steps[j][1]
            put("tensor", ("y", j), (("q", 2 * pair), ("q", 2 * pair + 1)), lambda: multiply(j))

        def t_turn(half):
            f = last_step[half]
            need = {4: ("n", f), 0: ("t", f)}.get(half[0], ("p", half))
            put("tensor", ("u", half), (need,), lambda: turn(*half))

        def t_piece(parity, i):
            j = steps.index((turned_v, 2 * turned_h + i // 2))
            put("tensor", ("e", parity, i), (("z", j), ("diag", 0), ("fill", 0), ("fill", 1)), lambda: convolve_turned(parity, i))

        def s_x(g):
            put("scalar", ("r", g), (("x", g),), lambda: regroup_x(g))

        def s_y(j):
            need = {4: ("sign", 2)}.get(kind(j), ("after", 0))
            put("scalar", ("z", j), (("y", j), need), lambda: leave_psum(j))

        def s_norm(j):
            put("scalar", ("n", j), (("t", j),), lambda: normalise(j))

        def s_out(half):
            put("scalar", ("s", half), (("u", half),), lambda: shuffle_out(*half))

        def s_relu():
            put("scalar", ("h", 0), tuple(("e", 0, i) for i in range(HALF)), relu_even)

        def v_x(g):
            put("vector", ("q", g), (("r", g),), lambda: quantise_x(g))

        def v_r(g):
            put("vector", ("r", g), (("x", g),), lambda: regroup_x_v(g))

        def v_first(j):
            if kind(j) in CONV:
                put("vector", ("t0", j), (("z", j),), lambda: add_tap(j, 0))
            if kind(j) == 4:
                put("vector", ("t0", j), (("z", j),), lambda: widen(j))

        def v_second(j):
            if kind(j) in CONV:
                put("vector", ("t", j), (("t0", j),), lambda: add_tap(j, 2))
            if kind(j) == 4:
                put("vector", ("t", j), (("t0", j),), lambda: choose(j))
            if kind(j) == 0:
                put("vector", ("t", j), (("z", j),), lambda: pool_plain(j))

        def v_pool(half):
            put("vector", ("p", half), (("m", half),), lambda: pool_pairs(*half))

        def v_merge():
            put("vector", ("s", TURNED), (("h", 0),) + tuple(("e", 1, i) for i in range(HALF)), merge_odd)

        def g_mend(half, engine="gpsimd"):
            pairs = [j for j in range(len(steps)) if (steps[j][0], steps[j][1] // 2) == half]
            put(engine, ("m", half), tuple(("t", j) for j in pairs) + (("bias", 0),), lambda: mend_edges(*half))

        HALVES = [(v, h) for v in range(NV) for h in range(2)]
        TAPPED = [half for half in HALVES if half[0] in CONV and half != TURNED]

        by_vector = ()
        t_x(0)
        put("tensor", ("par", 0), (), transpose_parameters)
        for g in (1, 2, 3):
            t_x(g)
        s_x(0)
        put("scalar", ("inv", 0), (("par", 0),), invert_std)
        put("scalar", ("copied", 0), (("par", 0),), copy_bias)
        for g in (1, 2, 3):
            if g in by_vector:
                pass
            else:
                s_x(g)
        put("vector", ("sum", 0), (("par", 0),), sum_taps)
        put("vector", ("count", 0), (("sum", 0), ("copied", 0)), count_bias)
        v_x(0)
        put("vector", ("scale", 0), (("inv", 0), ("count", 0)), scale_taps)
        v_x(1)
        put("vector", ("after", 0), (("scale", 0),), finish_offset)
        put("gpsimd", ("diag", 0), (("scale", 0),), make_diagonals)
        for g in (1, 2, 3):
            if g in by_vector:
                v_r(g)
        v_x(2)
        v_x(3)

        def v_small(name, part):
            call = {"bias": scale_bias, "fill": lambda: fill_padding(part), "sign": lambda: make_sign(part)}[name]
            need = ("copied", 0) if name == "fill" else ("after", 0)
            put("vector", (name, part), (need,), call)

        small = [("sign", 0), ("sign", 1), ("sign", 2), ("bias", 0), ("fill", 0), ("fill", 1)]
        n = len(steps)
        steps_last = max(TAPPED, key=lambda half: last_step[half])
        for j in range(-1, n + 6):
            if j + 1 < PAIRS - 1:
                t_y(j + 1)
                for g in (2 * j + 6, 2 * j + 7):
                    if g < G:
                        t_x(g)
            elif j + 1 == PAIRS - 1:
                t_y(j + 1)
                t_y(j + 2)
            elif j + 2 < n:
                t_y(j + 2)
            for half in HALVES:
                if half != TURNED and last_step[half] + {0: 1, 4: 2}.get(half[0], 4) == j:
                    t_turn(half)
            for k in range(2 * HALF):
                if ([6,7,9,10,12,13,15,16])[k] == j:
                    t_piece(k // HALF, k % HALF)
            if 0 <= j + 1 < n:
                s_y(j + 1)
            for g in (2 * j + 6, 2 * j + 7):
                if 4 <= g < G and g not in by_vector:
                    s_x(g)
            if 0 <= j - 1 < n and steps[j - 1][0] == 4:
                s_norm(j - 1)
            if j == 11:
                s_relu()
            for half in HALVES:
                if half != TURNED and last_step[half] + {0: 1, 4: 2}.get(half[0], 4) + 1 == j:
                    s_out(half)
            if 0 <= j < n and kind(j) != 4:
                v_first(j)
            if j + 1 < n and kind(j + 1) == 4 and j >= 0:
                v_first(j + 1)
            for half in TAPPED:
                if last_step[half] + 1 == j:
                    g_mend(half)
                if last_step[half] + 2 == j and False:
                    v_pool(half)
            if j >= 0 and small:
                v_small(*small[0])
                small = small[1:]
            if 0 <= j < n:
                v_second(j)
            if j >= 0 and small:
                v_small(*small[0])
                small = small[1:]
            for half in TAPPED:
                if last_step[half] + 2 == j and True:
                    v_pool(half)
            if j == 18:
                v_merge()
            for g in (2 * j + 6, 2 * j + 7):
                if 4 <= g < G and g in by_vector:
                    v_r(g)
            for g in (2 * j + 4, 2 * j + 5):
                if 4 <= g < G:
                    v_x(g)

        with tc.manual_schedule():
            written = set()
            places = {engine: 0 for engine in queues}
            left = sum(len(queues[engine]) for engine in queues)
            while left > 0:
                before = left
                for engine in ("tensor", "scalar", "vector", "gpsimd"):
                    place = places[engine]
                    if place < len(queues[engine]):
                        makes, needs, call = queues[engine][place]
                        if all(need in written for need in needs):
                            call()
                            written.add(makes)
                            places[engine] = place + 1
                            left -= 1
                assert left < before, str([(e, queues[e][places[e]][0:2]) for e in queues if places[e] < len(queues[e])])
